import numpy as np
import ml_dtypes


def mxq(x, axis, fmt="e4m3"):
    dtype, down = {"e4m3": (ml_dtypes.float8_e4m3fn, 7), "e5m2": (ml_dtypes.float8_e5m2, 14)}[fmt]
    v = np.moveaxis(np.asarray(x, np.float32).astype(ml_dtypes.bfloat16).astype(np.float64), axis, -1)
    blocks = v.reshape(v.shape[:-1] + (-1, 32))
    amax = np.abs(blocks).max(-1, keepdims=True)
    byte = np.maximum(np.where(amax > 0, np.frexp(amax)[1] - 1 + 127, 0) - down, 1)
    scale = np.exp2(byte - 127.0)
    codes = (blocks / scale).astype(np.float32).astype(dtype).astype(np.float64)
    return np.moveaxis((codes * scale).reshape(v.shape), -1, axis)


WIDE = False


def mx_kscale(k):
    if not WIDE:
        return np.ones(k)
    levels = np.array([10, -10, 5, -5, 0])
    if k % 512:
        return np.exp2(np.random.permutation(np.resize(levels, k // 32))).repeat(32)
    a = np.empty((k // 512, 16))
    for p in range(k // 512):
        a[p, :8] = np.random.permutation(np.resize(levels, 8))
        for g in range(8):
            far = levels[np.abs(levels - a[p, g]) >= 10]
            a[p, g + 8] = far[np.random.randint(len(far))]
    return np.exp2(a.ravel()).repeat(32)


BF16 = ml_dtypes.bfloat16


def bf(x):
    return np.asarray(x, np.float32).astype(BF16)


def f64(x):
    return np.asarray(x).astype(np.float64)


S, DIM, NH, NKV, HD, HID = 8192, 512, 8, 4, 32, 4096
EPS = 1e-6
ROPE_THETA = 10000.0


def rmsnorm(x, w):
    return x * (1.0 / np.sqrt(np.mean(x * x, axis=-1, keepdims=True) + EPS)) * w


def rope(t, cos, sin):
    te, to = t[..., 0::2], t[..., 1::2]
    c, s = cos[:, None, :], sin[:, None, :]
    re = te * c - to * s
    ro = te * s + to * c
    return np.stack([re, ro], axis=-1).reshape(t.shape)


def setup_inputs():
    s = mx_kscale(DIM)
    inv_freq = 1.0 / (ROPE_THETA ** (np.arange(0, HD, 2) / HD))
    ang = np.outer(np.arange(S), inv_freq)
    a = 1.0 / np.sqrt(DIM)
    return {"x": bf(np.random.standard_normal((S, DIM))),
            "freqs_cos": bf(np.cos(ang)),
            "freqs_sin": bf(np.sin(ang)),
            "wq": bf(np.random.standard_normal((NH * HD, DIM)) * 1.5 * a / s),
            "wk": bf(np.random.standard_normal((NKV * HD, DIM)) * 1.5 * a / s),
            "wv": bf(np.random.standard_normal((NKV * HD, DIM)) * a / s),
            "attn_norm_w": bf((1.0 + 0.1 * np.random.standard_normal(DIM)) * s)}


def reference(x, freqs_cos, freqs_sin, wq, wk, wv, attn_norm_w):
    hq = mxq(rmsnorm(f64(x), f64(attn_norm_w)), 1, "e4m3")
    q = (hq @ mxq(f64(wq), 1, "e4m3").T).reshape(S, NH, HD)
    k = (hq @ mxq(f64(wk), 1, "e4m3").T).reshape(S, NKV, HD)
    v = (hq @ mxq(f64(wv), 1, "e4m3").T).reshape(S, NKV, HD)
    c, sn = f64(freqs_cos), f64(freqs_sin)
    return rope(q, c, sn), rope(k, c, sn), v

@@ -1,0 +1,238 @@
+import concourse.mybir as mybir
+from concourse.masks import make_identity
+
+F32 = mybir.dt.float32
+BF16 = mybir.dt.bfloat16
+U32 = mybir.dt.uint32
+U8 = mybir.dt.uint8
+FP8X4 = mybir.dt.float8_e4m3fn_x4
+ACT = mybir.ActivationFunctionType
+ALU = mybir.AluOpType
+
+P = 128
+TOKENS = 8192
+DIM = 512
+HEAD = 32
+Q_COLS = 256
+KV_COLS = 128
+EPS = 1e-6
+
+TILES = TOKENS // P
+PAIR = 2
+GROUP = 4
+N_PAIRS = TILES // PAIR
+N_GROUPS = TILES // GROUP
+HALF = DIM // 2
+
+W_COLS = 2 * Q_COLS + 2 * KV_COLS + KV_COLS
+Q_PART = (0, 2 * Q_COLS)
+K_PART = (2 * Q_COLS, 2 * Q_COLS + 2 * KV_COLS)
+V_PART = (2 * Q_COLS + 2 * KV_COLS, W_COLS)
+
+FLOPS = 2 * TOKENS * DIM * (Q_COLS + 2 * KV_COLS)
+
+
+def tile_transformerblock_pa_t_kernel(
+    tc, x, freqs_cos, freqs_sin, wq, wk, wv, attn_norm_w, out_0, out_1, out_2
+):
+    nc = tc.nc
+
+    x_view = x.rearrange("(p t) k -> p t k", t=TILES)
+    cos_view = freqs_cos.rearrange("(p t) j -> p t j", t=TILES)
+    sin_view = freqs_sin.rearrange("(p t) j -> p t j", t=TILES)
+    q_view = out_0.rearrange("(p t) h d -> p t (h d)", t=TILES)
+    k_view = out_1.rearrange("(p t) h d -> p t (h d)", t=TILES)
+    v_view = out_2.rearrange("(p t) h d -> p t (h d)", t=TILES)
+
+    with (
+        tc.tile_pool(name="const", bufs=1) as const,
+        tc.tile_pool(name="xin", bufs=N_GROUPS) as xin,
+        tc.tile_pool(name="stats", bufs=4) as stats,
+        tc.tile_pool(name="work", bufs=3) as work,
+        tc.tile_pool(name="outs", bufs=3) as outs,
+        tc.psum_pool(name="ps_gain", bufs=1) as ps_gain,
+        tc.psum_pool(name="ps_t", bufs=2) as ps_t,
+        tc.psum_pool(name="ps_q", bufs=3) as ps_q,
+        tc.psum_pool(name="ps_k", bufs=1) as ps_k,
+        tc.psum_pool(name="ps_v", bufs=1) as ps_v,
+    ):
+        w_raw = const.tile([P, 4, DIM], BF16)
+        nc.sync.dma_start(out=w_raw[:, 0:2, :], in_=wq.rearrange("(b p) k -> p b k", p=P))
+        nc.sync.dma_start(out=w_raw[:, 2, :], in_=wk)
+        nc.sync.dma_start(out=w_raw[:, 3, :], in_=wv)
+        gain_row = const.tile([P, DIM], BF16)
+        nc.vector.memset(gain_row[:], 0.0)
+        nc.sync.dma_start(out=gain_row[0:1, :], in_=attn_norm_w.rearrange("(o k) -> o k", o=1))
+        cos_sb = const.tile([P, TILES, HEAD // 2], BF16)
+        sin_sb = const.tile([P, TILES, HEAD // 2], BF16)
+        x_groups = []
+        for g in range(N_GROUPS):
+            x_sb = xin.tile([P, GROUP, DIM], BF16, name="x_sb")
+            nc.sync.dma_start(out=x_sb[:], in_=x_view[:, g * GROUP : (g + 1) * GROUP, :])
+            x_groups.append(x_sb)
+            if g == 0:
+                nc.sync.dma_start(out=cos_sb[:], in_=cos_view)
+                nc.sync.dma_start(out=sin_sb[:], in_=sin_view)
+
+        ident = const.tile([P, P], F32)
+        make_identity(nc, ident[:])
+        swap = const.tile([P, P], F32)
+        ident_pairs = ident[:].rearrange("p (m e) -> p m e", e=2)
+        swap_pairs = swap[:].rearrange("p (m e) -> p m e", e=2)
+        nc.vector.tensor_copy(out=swap_pairs[:, :, 0], in_=ident_pairs[:, :, 1])
+        nc.vector.tensor_copy(out=swap_pairs[:, :, 1], in_=ident_pairs[:, :, 0])
+        eps = const.tile([P, 1], F32)
+        nc.vector.memset(eps[:], EPS)
+        ones = const.tile([P, P], BF16)
+        nc.vector.memset(ones[:], 1.0)
+
+        gain = ps_gain.tile([P, DIM], F32)
+        nc.tensor.matmul(gain[:], lhsT=ones[:], rhs=gain_row[:], start=True, stop=True)
+
+        trig = const.tile([P, TILES, 2, HEAD], BF16)
+        trig_pairs = trig[:].rearrange("p t c (j e) -> p t c j e", e=2)
+        nc.gpsimd.tensor_scalar(trig_pairs[:, :, 0, :, 0], cos_sb[:], 1.0, 0.0, op0=ALU.mult, op1=ALU.add)
+        nc.gpsimd.tensor_scalar(trig_pairs[:, :, 0, :, 1], cos_sb[:], 1.0, 0.0, op0=ALU.mult, op1=ALU.add)
+        nc.gpsimd.tensor_scalar(trig_pairs[:, :, 1, :, 0], sin_sb[:], -1.0, 0.0, op0=ALU.mult, op1=ALU.add)
+        nc.gpsimd.tensor_scalar(trig_pairs[:, :, 1, :, 1], sin_sb[:], 1.0, 0.0, op0=ALU.mult, op1=ALU.add)
+
+        w_grouped = const.tile([P, W_COLS * 4], BF16, align_bytes=64)
+        w_words = w_grouped[:].bitcast(F32).rearrange("p (n u) -> p n u", u=2)
+        w_blocks = [(0, ident), (1, ident), (0, swap), (1, swap), (2, ident), (2, swap), (3, ident)]
+        for slot, (block, perm) in enumerate(w_blocks):
+            w_t = ps_t.tile([P, 2, P], F32, tag="turned")
+            for u in range(2):
+                nc.tensor.transpose(
+                    w_t[:, u, :], w_raw[:, block, :].bitcast(F32)[:, u : 2 * P : 2], perm[:]
+                )
+            nc.vector.tensor_copy(
+                out=w_words[:, slot * P : (slot + 1) * P, :], in_=w_t[:].rearrange("p u n -> p n u")
+            )
+        w_codes = const.tile([P, W_COLS], U32, align_bytes=64)
+        w_scales = const.tile([P, W_COLS], U8, align_bytes=64)
+        for lo, hi in (Q_PART, K_PART, V_PART):
+            nc.vector.quantize_mx(
+                out=w_codes[:, lo:hi].bitcast(FP8X4),
+                scales=w_scales[:, lo:hi],
+                in_=w_grouped[:, 4 * lo : 4 * hi],
+            )
+
+        rstd_of_group = {}
+        h_of_pair = {}
+        codes_of_pair = {}
+        banks_of_pair = {}
+        outs_of_group = {}
+
+        def statistics(g):
+            sumsq = stats.tile([P, GROUP], F32, name="sumsq")
+            for i in range(GROUP):
+                squares = stats.tile([P, DIM], BF16, name="squares")
+                nc.scalar.activation(
+                    out=squares[:], in_=x_groups[g][:, i, :], func=ACT.Square,
+                    accum_out=sumsq[:, i : i + 1],
+                )
+            std = stats.tile([P, GROUP], F32, name="std")
+            nc.scalar.activation(out=std[:], in_=sumsq[:], func=ACT.Sqrt, bias=eps[:], scale=1.0 / DIM)
+            rstd = stats.tile([P, GROUP], F32, name="rstd")
+            nc.vector.reciprocal(out=rstd[:], in_=std[:])
+            rstd_of_group[g] = rstd
+
+        def normalise_and_turn(pair):
+            g, first = divmod(pair * PAIR, GROUP)
+            h = work.tile([P, PAIR, DIM], BF16, name="h")
+            for a in range(PAIR):
+                nc.vector.scalar_tensor_tensor(
+                    out=h[:, a, :], in0=x_groups[g][:, first + a, :],
+                    scalar=rstd_of_group[g][:, first + a : first + a + 1], in1=gain[:],
+                    op0=ALU.mult, op1=ALU.mult,
+                )
+            turned = ps_t.tile([P, PAIR, 2, P], F32, tag="turned")
+            for a in range(PAIR):
+                for u in range(2):
+                    nc.tensor.transpose(
+                        turned[:, a, u, :], h[:, a, :].bitcast(F32)[:, u : 2 * P : 2], ident[:]
+                    )
+            h_grouped = work.tile([P, PAIR * P * 4], BF16, name="h_grouped", align_bytes=64)
+            nc.scalar.copy(
+                out=h_grouped[:].bitcast(F32).rearrange("p (a r u) -> p a r u", a=PAIR, u=2),
+                in_=turned[:].rearrange("p a u r -> p a r u"),
+            )
+            h_of_pair[pair] = h_grouped
+
+        def quantise_and_project(pair):
+            h_codes = work.tile([P, PAIR * P], U32, name="h_codes", align_bytes=64)
+            h_scales = work.tile([P, PAIR * P], U8, name="h_scales", align_bytes=64)
+            nc.vector.quantize_mx(
+                out=h_codes[:].bitcast(FP8X4), scales=h_scales[:], in_=h_of_pair.pop(pair)[:]
+            )
+            k_bank = ps_k.tile([P, PAIR, 2 * KV_COLS], F32, name="k_bank")
+            v_bank = ps_v.tile([P, PAIR, KV_COLS], F32, name="v_bank")
+            q_banks = []
+            for a in range(PAIR):
+                q_bank = ps_q.tile([P, 2 * Q_COLS], F32, name="q_bank")
+                q_banks.append(q_bank)
+                tokens = slice(a * P, (a + 1) * P)
+                for dest, (lo, hi) in ((q_bank[:], Q_PART), (k_bank[:, a, :], K_PART), (v_bank[:, a, :], V_PART)):
+                    nc.tensor.matmul_mx(
+                        out=dest,
+                        lhsT=h_codes[:, tokens].bitcast(FP8X4),
+                        lhsT_scale=h_scales[:, tokens],
+                        rhs=w_codes[:, lo:hi].bitcast(FP8X4),
+                        rhs_scale=w_scales[:, lo:hi],
+                        start=True,
+                        stop=True,
+                    )
+            banks_of_pair[pair] = (q_banks, k_bank, v_bank)
+
+        def rope(pair):
+            g, first = divmod(pair * PAIR, GROUP)
+            if first == 0:
+                q_out = outs.tile([P, GROUP, Q_COLS], F32, name="q_out")
+                k_out = outs.tile([P, GROUP, KV_COLS], F32, name="k_out")
+                v_out = outs.tile([P, GROUP, KV_COLS], F32, name="v_out")
+                outs_of_group[g] = (q_out, k_out, v_out)
+            q_out, k_out, v_out = outs_of_group[g]
+            q_banks, k_bank, v_bank = banks_of_pair.pop(pair)
+            here = slice(first, first + PAIR)
+            t0 = pair * PAIR
+
+            nc.scalar.copy(out=v_out[:, here, :], in_=v_bank[:])
+
+            k_prod = work.tile([P, PAIR, 2, KV_COLS], F32, name="k_prod")
+            nc.vector.tensor_tensor(
+                out=k_prod[:].rearrange("p a c (h d) -> p (a c) h d", d=HEAD),
+                in0=k_bank[:].rearrange("p a (c h d) -> p (a c) h d", c=2, d=HEAD),
+                in1=trig[:, t0 : t0 + PAIR, :, :].rearrange("p t c d -> p (t c) d").unsqueeze(2)
+                .to_broadcast([P, PAIR * 2, KV_COLS // HEAD, HEAD]),
+                op=ALU.mult,
+            )
+            q_prod = work.tile([P, PAIR, 2, Q_COLS], F32, name="q_prod")
+            for a in range(PAIR):
+                nc.vector.tensor_tensor(
+                    out=q_prod[:, a, :, :].rearrange("p c (h d) -> p c h d", d=HEAD),
+                    in0=q_banks[a][:].rearrange("p (c h d) -> p c h d", c=2, d=HEAD),
+                    in1=trig[:, t0 + a, :, :].unsqueeze(2).to_broadcast([P, 2, Q_COLS // HEAD, HEAD]),
+                    op=ALU.mult,
+                )
+            nc.gpsimd.tensor_tensor(
+                out=k_out[:, here, :], in0=k_prod[:, :, 0, :], in1=k_prod[:, :, 1, :], op=ALU.add
+            )
+            nc.gpsimd.tensor_tensor(
+                out=q_out[:, here, :], in0=q_prod[:, :, 0, :], in1=q_prod[:, :, 1, :], op=ALU.add
+            )
+            if first + PAIR == GROUP:
+                tiles = slice(g * GROUP, (g + 1) * GROUP)
+                nc.sync.dma_start(out=q_view[:, tiles, :], in_=q_out[:])
+                nc.sync.dma_start(out=k_view[:, tiles, :], in_=k_out[:])
+                nc.sync.dma_start(out=v_view[:, tiles, :], in_=v_out[:])
+
+        statistics(0)
+        for step in range(N_PAIRS + 2):
+            if step % (GROUP // PAIR) == 0 and step // (GROUP // PAIR) + 1 < N_GROUPS:
+                statistics(step // (GROUP // PAIR) + 1)
+            if step < N_PAIRS:
+                normalise_and_turn(step)
+            if 0 <= step - 1 < N_PAIRS:
+                quantise_and_project(step - 1)
+            if 0 <= step - 2:
+                rope(step - 2)

@@ -13,8 +13,13 @@ P = 128
 TOKENS = 8192
 DIM = 512
 HEAD = 32
-Q_COLS = 256
-KV_COLS = 128
+ANGLES = HEAD // 2
+Q_HEADS = 8
+K_HEADS = 4
+HEADS = Q_HEADS + K_HEADS
+Q_COLS = Q_HEADS * HEAD
+KV_COLS = K_HEADS * HEAD
+HALF = HEADS * ANGLES
 EPS = 1e-6
 
 TILES = TOKENS // P
@@ -22,12 +27,9 @@ PAIR = 2
 GROUP = 4
 N_PAIRS = TILES // PAIR
 N_GROUPS = TILES // GROUP
-HALF = DIM // 2
 
-W_COLS = 2 * Q_COLS + 2 * KV_COLS + KV_COLS
-Q_PART = (0, 2 * Q_COLS)
-K_PART = (2 * Q_COLS, 2 * Q_COLS + 2 * KV_COLS)
-V_PART = (2 * Q_COLS + 2 * KV_COLS, W_COLS)
+ODD_Q, ODD_K, EVEN_Q, EVEN_K, V_AT = 0, 128, 192, 320, 384
+W_COLS = 512
 
 FLOPS = 2 * TOKENS * DIM * (Q_COLS + 2 * KV_COLS)
 
@@ -43,196 +45,267 @@ def tile_transformerblock_pa_t_kernel(
     q_view = out_0.rearrange("(p t) h d -> p t (h d)", t=TILES)
     k_view = out_1.rearrange("(p t) h d -> p t (h d)", t=TILES)
     v_view = out_2.rearrange("(p t) h d -> p t (h d)", t=TILES)
+    wk_view = wk.rearrange("(n e) k -> n e k", e=2)
 
     with (
         tc.tile_pool(name="const", bufs=1) as const,
         tc.tile_pool(name="xin", bufs=N_GROUPS) as xin,
         tc.tile_pool(name="stats", bufs=4) as stats,
         tc.tile_pool(name="work", bufs=3) as work,
-        tc.tile_pool(name="outs", bufs=3) as outs,
+        tc.tile_pool(name="outs", bufs=4) as outs,
         tc.psum_pool(name="ps_gain", bufs=1) as ps_gain,
         tc.psum_pool(name="ps_t", bufs=2) as ps_t,
-        tc.psum_pool(name="ps_q", bufs=3) as ps_q,
-        tc.psum_pool(name="ps_k", bufs=1) as ps_k,
+        tc.psum_pool(name="ps_eo", bufs=3) as ps_eo,
+        tc.psum_pool(name="ps_sum", bufs=1) as ps_sum,
         tc.psum_pool(name="ps_v", bufs=1) as ps_v,
+        tc.manual_schedule(),
     ):
         w_raw = const.tile([P, 4, DIM], BF16)
-        nc.sync.dma_start(out=w_raw[:, 0:2, :], in_=wq.rearrange("(b p) k -> p b k", p=P))
-        nc.sync.dma_start(out=w_raw[:, 2, :], in_=wk)
+        nc.sync.dma_start(out=w_raw[:, 0:2, :], in_=wq.rearrange("(n e) k -> n e k", e=2))
+        nc.sync.dma_start(out=w_raw[0:64, 2, :], in_=wk_view[:, 0, :])
+        nc.sync.dma_start(out=w_raw[64:128, 2, :], in_=wk_view[:, 1, :])
         nc.sync.dma_start(out=w_raw[:, 3, :], in_=wv)
         gain_row = const.tile([P, DIM], BF16)
         nc.vector.memset(gain_row[:], 0.0)
-        nc.sync.dma_start(out=gain_row[0:1, :], in_=attn_norm_w.rearrange("(o k) -> o k", o=1))
-        cos_sb = const.tile([P, TILES, HEAD // 2], BF16)
-        sin_sb = const.tile([P, TILES, HEAD // 2], BF16)
         x_groups = []
         for g in range(N_GROUPS):
             x_sb = xin.tile([P, GROUP, DIM], BF16, name="x_sb")
-            nc.sync.dma_start(out=x_sb[:], in_=x_view[:, g * GROUP : (g + 1) * GROUP, :])
             x_groups.append(x_sb)
-            if g == 0:
+        nc.sync.dma_start(out=x_groups[0][:, 0:PAIR, :], in_=x_view[:, 0:PAIR, :])
+        nc.sync.dma_start(out=gain_row[0:1, :], in_=attn_norm_w.rearrange("(o k) -> o k", o=1))
+        nc.sync.dma_start(out=x_groups[0][:, PAIR:GROUP, :], in_=x_view[:, PAIR:GROUP, :])
+        cos_sb = const.tile([P, TILES, ANGLES], BF16)
+        sin_sb = const.tile([P, TILES, ANGLES], BF16)
+        for g in range(1, N_GROUPS):
+            nc.sync.dma_start(out=x_groups[g][:], in_=x_view[:, g * GROUP : (g + 1) * GROUP, :])
+            if g == 1:
                 nc.sync.dma_start(out=cos_sb[:], in_=cos_view)
                 nc.sync.dma_start(out=sin_sb[:], in_=sin_view)
 
         ident = const.tile([P, P], F32)
         make_identity(nc, ident[:])
-        swap = const.tile([P, P], F32)
-        ident_pairs = ident[:].rearrange("p (m e) -> p m e", e=2)
-        swap_pairs = swap[:].rearrange("p (m e) -> p m e", e=2)
-        nc.vector.tensor_copy(out=swap_pairs[:, :, 0], in_=ident_pairs[:, :, 1])
-        nc.vector.tensor_copy(out=swap_pairs[:, :, 1], in_=ident_pairs[:, :, 0])
         eps = const.tile([P, 1], F32)
         nc.vector.memset(eps[:], EPS)
         ones = const.tile([P, P], BF16)
         nc.vector.memset(ones[:], 1.0)
+        warm = const.tile([P, 1], F32)
+        nc.scalar.activation(out=warm[:], in_=eps[:], func=ACT.Sqrt)
 
-        gain = ps_gain.tile([P, DIM], F32)
-        nc.tensor.matmul(gain[:], lhsT=ones[:], rhs=gain_row[:], start=True, stop=True)
+        mix = const.tile([P, TILES, ANGLES, 2], F32)
+        minus_sin = const.tile([P, TILES, ANGLES], BF16)
 
-        trig = const.tile([P, TILES, 2, HEAD], BF16)
-        trig_pairs = trig[:].rearrange("p t c (j e) -> p t c j e", e=2)
-        nc.gpsimd.tensor_scalar(trig_pairs[:, :, 0, :, 0], cos_sb[:], 1.0, 0.0, op0=ALU.mult, op1=ALU.add)
-        nc.gpsimd.tensor_scalar(trig_pairs[:, :, 0, :, 1], cos_sb[:], 1.0, 0.0, op0=ALU.mult, op1=ALU.add)
-        nc.gpsimd.tensor_scalar(trig_pairs[:, :, 1, :, 0], sin_sb[:], -1.0, 0.0, op0=ALU.mult, op1=ALU.add)
-        nc.gpsimd.tensor_scalar(trig_pairs[:, :, 1, :, 1], sin_sb[:], 1.0, 0.0, op0=ALU.mult, op1=ALU.add)
+        def build_mix(lo, hi):
+            nc.gpsimd.tensor_scalar(
+                minus_sin[:, lo:hi, :], sin_sb[:, lo:hi, :], -1.0, 0.0, op0=ALU.mult, op1=ALU.add
+            )
+            nc.gpsimd.tensor_tensor(
+                out=mix[:, lo:hi, :, 0], in0=minus_sin[:, lo:hi, :], in1=cos_sb[:, lo:hi, :], op=ALU.subtract
+            )
+            nc.gpsimd.tensor_tensor(
+                out=mix[:, lo:hi, :, 1], in0=sin_sb[:, lo:hi, :], in1=cos_sb[:, lo:hi, :], op=ALU.subtract
+            )
 
         w_grouped = const.tile([P, W_COLS * 4], BF16, align_bytes=64)
         w_words = w_grouped[:].bitcast(F32).rearrange("p (n u) -> p n u", u=2)
-        w_blocks = [(0, ident), (1, ident), (0, swap), (1, swap), (2, ident), (2, swap), (3, ident)]
-        for slot, (block, perm) in enumerate(w_blocks):
-            w_t = ps_t.tile([P, 2, P], F32, tag="turned")
-            for u in range(2):
-                nc.tensor.transpose(
-                    w_t[:, u, :], w_raw[:, block, :].bitcast(F32)[:, u : 2 * P : 2], perm[:]
-                )
-            nc.vector.tensor_copy(
-                out=w_words[:, slot * P : (slot + 1) * P, :], in_=w_t[:].rearrange("p u n -> p n u")
-            )
+        w_places = [
+            [(0, P, EVEN_Q)],
+            [(0, P, ODD_Q)],
+            [(0, 64, EVEN_K), (64, P, ODD_K)],
+            [(0, P, V_AT)],
+        ]
+        for half in range(2):
+            w_t = ps_t.tile([P, 2, 2, P], F32, tag="turned")
+            for a in range(2):
+                for u in range(2):
+                    nc.tensor.transpose(
+                        w_t[:, a, u, :], w_raw[:, 2 * half + a, :].bitcast(F32)[:, u : 2 * P : 2], ident[:]
+                    )
+            for a in range(2):
+                for lo, hi, at in w_places[2 * half + a]:
+                    nc.vector.tensor_copy(
+                        out=w_words[:, at : at + hi - lo, :], in_=w_t[:, a, :, lo:hi].rearrange("p u n -> p n u")
+                    )
+        gain = ps_gain.tile([P, DIM], F32)
+        nc.tensor.matmul(gain[:], lhsT=ones[:], rhs=gain_row[:], start=True, stop=True)
         w_codes = const.tile([P, W_COLS], U32, align_bytes=64)
         w_scales = const.tile([P, W_COLS], U8, align_bytes=64)
-        for lo, hi in (Q_PART, K_PART, V_PART):
-            nc.vector.quantize_mx(
-                out=w_codes[:, lo:hi].bitcast(FP8X4),
-                scales=w_scales[:, lo:hi],
-                in_=w_grouped[:, 4 * lo : 4 * hi],
-            )
+        nc.vector.quantize_mx(out=w_codes[:].bitcast(FP8X4), scales=w_scales[:], in_=w_grouped[:])
 
-        rstd_of_group = {}
-        h_of_pair = {}
+        sums_of_batch = {}
+        std_of_batch = {}
+        rstd_of_tile = {}
+        turned_of_pair = {}
         codes_of_pair = {}
+        h_of_pair = {}
         banks_of_pair = {}
         outs_of_group = {}
+        products_of_group = {}
 
-        def statistics(g):
-            sumsq = stats.tile([P, GROUP], F32, name="sumsq")
-            for i in range(GROUP):
-                squares = stats.tile([P, DIM], BF16, name="squares")
+        def batch_of(pair):
+            t0 = pair * PAIR
+            if t0 < GROUP:
+                return t0, PAIR
+            return t0 - t0 % GROUP, GROUP
+
+        def squares(pair):
+            first, count = batch_of(pair)
+            if pair * PAIR == first:
+                sumsq = stats.tile([P, GROUP], F32, name="sumsq")
+                sums_of_batch[first] = sumsq
+            for t in range(pair * PAIR, (pair + 1) * PAIR):
+                g, at = divmod(t, GROUP)
+                junk = stats.tile([P, DIM], BF16, name="junk")
                 nc.scalar.activation(
-                    out=squares[:], in_=x_groups[g][:, i, :], func=ACT.Square,
-                    accum_out=sumsq[:, i : i + 1],
+                    out=junk[:], in_=x_groups[g][:, at, :], func=ACT.Square,
+                    accum_out=sums_of_batch[first][:, t - first : t - first + 1],
                 )
-            std = stats.tile([P, GROUP], F32, name="std")
-            nc.scalar.activation(out=std[:], in_=sumsq[:], func=ACT.Sqrt, bias=eps[:], scale=1.0 / DIM)
-            rstd = stats.tile([P, GROUP], F32, name="rstd")
-            nc.vector.reciprocal(out=rstd[:], in_=std[:])
-            rstd_of_group[g] = rstd
+            if (pair + 1) * PAIR == first + count:
+                std = stats.tile([P, GROUP], F32, name="std")
+                nc.scalar.activation(
+                    out=std[:, 0:count], in_=sums_of_batch.pop(first)[:, 0:count], func=ACT.Sqrt,
+                    bias=eps[:], scale=1.0 / DIM,
+                )
+                std_of_batch[first] = std
 
-        def normalise_and_turn(pair):
-            g, first = divmod(pair * PAIR, GROUP)
+        def normalise(pair):
+            first, count = batch_of(pair)
+            if pair * PAIR == first:
+                rstd = stats.tile([P, GROUP], F32, name="rstd")
+                nc.vector.reciprocal(out=rstd[:, 0:count], in_=std_of_batch.pop(first)[:, 0:count])
+                for i in range(count):
+                    rstd_of_tile[first + i] = rstd[:, i : i + 1]
             h = work.tile([P, PAIR, DIM], BF16, name="h")
-            for a in range(PAIR):
-                nc.vector.scalar_tensor_tensor(
-                    out=h[:, a, :], in0=x_groups[g][:, first + a, :],
-                    scalar=rstd_of_group[g][:, first + a : first + a + 1], in1=gain[:],
-                    op0=ALU.mult, op1=ALU.mult,
-                )
             turned = ps_t.tile([P, PAIR, 2, P], F32, tag="turned")
             for a in range(PAIR):
+                t = pair * PAIR + a
+                g, at = divmod(t, GROUP)
+                nc.vector.scalar_tensor_tensor(
+                    out=h[:, a, :], in0=x_groups[g][:, at, :], scalar=rstd_of_tile.pop(t), in1=gain[:],
+                    op0=ALU.mult, op1=ALU.mult,
+                )
                 for u in range(2):
                     nc.tensor.transpose(
                         turned[:, a, u, :], h[:, a, :].bitcast(F32)[:, u : 2 * P : 2], ident[:]
                     )
+            turned_of_pair[pair] = turned
+
+        def words(pair):
             h_grouped = work.tile([P, PAIR * P * 4], BF16, name="h_grouped", align_bytes=64)
             nc.scalar.copy(
                 out=h_grouped[:].bitcast(F32).rearrange("p (a r u) -> p a r u", a=PAIR, u=2),
-                in_=turned[:].rearrange("p a u r -> p a r u"),
+                in_=turned_of_pair.pop(pair)[:].rearrange("p a u r -> p a r u"),
             )
             h_of_pair[pair] = h_grouped
 
-        def quantise_and_project(pair):
-            h_codes = work.tile([P, PAIR * P], U32, name="h_codes", align_bytes=64)
-            h_scales = work.tile([P, PAIR * P], U8, name="h_scales", align_bytes=64)
-            nc.vector.quantize_mx(
-                out=h_codes[:].bitcast(FP8X4), scales=h_scales[:], in_=h_of_pair.pop(pair)[:]
-            )
-            k_bank = ps_k.tile([P, PAIR, 2 * KV_COLS], F32, name="k_bank")
-            v_bank = ps_v.tile([P, PAIR, KV_COLS], F32, name="v_bank")
-            q_banks = []
-            for a in range(PAIR):
-                q_bank = ps_q.tile([P, 2 * Q_COLS], F32, name="q_bank")
-                q_banks.append(q_bank)
-                tokens = slice(a * P, (a + 1) * P)
-                for dest, (lo, hi) in ((q_bank[:], Q_PART), (k_bank[:, a, :], K_PART), (v_bank[:, a, :], V_PART)):
-                    nc.tensor.matmul_mx(
-                        out=dest,
-                        lhsT=h_codes[:, tokens].bitcast(FP8X4),
-                        lhsT_scale=h_scales[:, tokens],
-                        rhs=w_codes[:, lo:hi].bitcast(FP8X4),
-                        rhs_scale=w_scales[:, lo:hi],
-                        start=True,
-                        stop=True,
-                    )
-            banks_of_pair[pair] = (q_banks, k_bank, v_bank)
+        def quantise(pair):
+            codes = work.tile([P, PAIR * P], U32, name="codes", align_bytes=64)
+            scales = work.tile([P, PAIR * P], U8, name="scales", align_bytes=64)
+            nc.vector.quantize_mx(out=codes[:].bitcast(FP8X4), scales=scales[:], in_=h_of_pair.pop(pair)[:])
+            codes_of_pair[pair] = (codes, scales)
 
-        def rope(pair):
+        def project(pair):
+            codes, scales = codes_of_pair.pop(pair)
+
+            def one_pass(dest, a, lo, hi, start, stop):
+                tokens = slice(a * P, (a + 1) * P)
+                nc.tensor.matmul_mx(
+                    out=dest,
+                    lhsT=codes[:, tokens].bitcast(FP8X4),
+                    lhsT_scale=scales[:, tokens],
+                    rhs=w_codes[:, lo:hi].bitcast(FP8X4),
+                    rhs_scale=w_scales[:, lo:hi],
+                    start=start,
+                    stop=stop,
+                )
+
+            sums = ps_sum.tile([P, PAIR, 256], F32, name="sums")
+            v_bank = ps_v.tile([P, PAIR, KV_COLS], F32, name="v_bank")
+            members = []
+            for a in range(PAIR):
+                one_pass(sums[:, a, :], a, 0, 256, True, False)
+                one_pass(sums[:, a, :], a, HALF, HALF + 256, False, True)
+            for a in range(PAIR):
+                bank = ps_eo.tile([P, 512], F32, name="bank")
+                members.append(bank)
+                one_pass(bank[:, 0:256], a, 0, 256, True, True)
+                one_pass(bank[:, 256 : 2 * HALF], a, 256, 2 * HALF, True, True)
+                one_pass(v_bank[:, a, :], a, V_AT, V_AT + KV_COLS, True, True)
+            banks_of_pair[pair] = (sums, v_bank, members)
+
+        def copy_v(pair):
             g, first = divmod(pair * PAIR, GROUP)
             if first == 0:
                 q_out = outs.tile([P, GROUP, Q_COLS], F32, name="q_out")
                 k_out = outs.tile([P, GROUP, KV_COLS], F32, name="k_out")
                 v_out = outs.tile([P, GROUP, KV_COLS], F32, name="v_out")
                 outs_of_group[g] = (q_out, k_out, v_out)
-            q_out, k_out, v_out = outs_of_group[g]
-            q_banks, k_bank, v_bank = banks_of_pair.pop(pair)
-            here = slice(first, first + PAIR)
+            nc.scalar.copy(out=outs_of_group[g][2][:, first : first + PAIR, :], in_=banks_of_pair[pair][1][:])
+
+        def common_products(pair):
             t0 = pair * PAIR
-
-            nc.scalar.copy(out=v_out[:, here, :], in_=v_bank[:])
-
-            k_prod = work.tile([P, PAIR, 2, KV_COLS], F32, name="k_prod")
+            first = t0 % GROUP
+            if first == 0:
+                common = work.tile([P, GROUP, HALF], F32, name="common")
+                own = work.tile([P, GROUP, 2 * HALF], F32, name="own")
+                products_of_group[t0 // GROUP] = (common, own)
+            common = products_of_group[t0 // GROUP][0]
             nc.vector.tensor_tensor(
-                out=k_prod[:].rearrange("p a c (h d) -> p (a c) h d", d=HEAD),
-                in0=k_bank[:].rearrange("p a (c h d) -> p (a c) h d", c=2, d=HEAD),
-                in1=trig[:, t0 : t0 + PAIR, :, :].rearrange("p t c d -> p (t c) d").unsqueeze(2)
-                .to_broadcast([P, PAIR * 2, KV_COLS // HEAD, HEAD]),
+                out=common[:, first : first + PAIR, :].rearrange("p a (h j) -> p a h j", j=ANGLES),
+                in0=banks_of_pair[pair][0][:, :, 0:HALF].rearrange("p a (h j) -> p a h j", j=ANGLES),
+                in1=cos_sb[:, t0 : t0 + PAIR, :].unsqueeze(2).to_broadcast([P, PAIR, HEADS, ANGLES]),
                 op=ALU.mult,
             )
-            q_prod = work.tile([P, PAIR, 2, Q_COLS], F32, name="q_prod")
-            for a in range(PAIR):
-                nc.vector.tensor_tensor(
-                    out=q_prod[:, a, :, :].rearrange("p c (h d) -> p c h d", d=HEAD),
-                    in0=q_banks[a][:].rearrange("p (c h d) -> p c h d", c=2, d=HEAD),
-                    in1=trig[:, t0 + a, :, :].unsqueeze(2).to_broadcast([P, 2, Q_COLS // HEAD, HEAD]),
-                    op=ALU.mult,
-                )
-            nc.gpsimd.tensor_tensor(
-                out=k_out[:, here, :], in0=k_prod[:, :, 0, :], in1=k_prod[:, :, 1, :], op=ALU.add
+
+        def own_products(tile):
+            g, at = divmod(tile, GROUP)
+            bank = banks_of_pair[tile // PAIR][2][tile % PAIR]
+            nc.vector.tensor_tensor(
+                out=products_of_group[g][1][:, at, :].rearrange("p (h j e) -> p h j e", h=HEADS, e=2),
+                in0=bank[:, 0 : 2 * HALF].rearrange("p (e h j) -> p h j e", e=2, h=HEADS),
+                in1=mix[:, tile, :, :].unsqueeze(1).to_broadcast([P, HEADS, ANGLES, 2]),
+                op=ALU.mult,
             )
+
+        def add_products(out, own, common):
+            tiles, pairs = common.shape[1], common.shape[2]
             nc.gpsimd.tensor_tensor(
-                out=q_out[:, here, :], in0=q_prod[:, :, 0, :], in1=q_prod[:, :, 1, :], op=ALU.add
+                out=out.rearrange("p a (n e) -> p a n e", e=2),
+                in0=own.rearrange("p a (n e) -> p a n e", e=2),
+                in1=common.unsqueeze(3).to_broadcast([P, tiles, pairs, 2]),
+                op=ALU.add,
             )
+
+        def add_and_store(pair):
+            g, first = divmod(pair * PAIR, GROUP)
+            q_out, k_out, v_out = outs_of_group[g]
+            common, own = products_of_group[g]
+            q_half = Q_COLS // 2
+            here = slice(first, first + PAIR)
+            add_products(q_out[:, here, :], own[:, here, 0:Q_COLS], common[:, here, 0:q_half])
             if first + PAIR == GROUP:
+                add_products(k_out[:], own[:, :, Q_COLS : 2 * HALF], common[:, :, q_half:HALF])
                 tiles = slice(g * GROUP, (g + 1) * GROUP)
+                nc.sync.dma_start(out=v_view[:, tiles, :], in_=v_out[:])
                 nc.sync.dma_start(out=q_view[:, tiles, :], in_=q_out[:])
                 nc.sync.dma_start(out=k_view[:, tiles, :], in_=k_out[:])
-                nc.sync.dma_start(out=v_view[:, tiles, :], in_=v_out[:])
 
-        statistics(0)
-        for step in range(N_PAIRS + 2):
-            if step % (GROUP // PAIR) == 0 and step // (GROUP // PAIR) + 1 < N_GROUPS:
-                statistics(step // (GROUP // PAIR) + 1)
-            if step < N_PAIRS:
-                normalise_and_turn(step)
-            if 0 <= step - 1 < N_PAIRS:
-                quantise_and_project(step - 1)
-            if 0 <= step - 2:
-                rope(step - 2)
+        def on(stage, pair):
+            return stage(pair) if 0 <= pair < N_PAIRS else None
+
+        for s in range(-5, N_PAIRS):
+            if s == -3:
+                build_mix(0, 16)
+            elif s == -1:
+                build_mix(16, TILES)
+            on(copy_v, s)
+            on(common_products, s)
+            if 0 <= s:
+                own_products(s * PAIR)
+            on(quantise, s + 1)
+            if 0 <= s:
+                own_products(s * PAIR + 1)
+            on(project, s + 1)
+            on(squares, s + 5)
+            on(words, s + 2)
+            on(normalise, s + 3)
+            on(add_and_store, s)

@@ -219,7 +219,7 @@ def tile_transformerblock_pa_t_kernel(
                 )
 
             sums = ps_sum.tile([P, PAIR, 256], F32, name="sums")
-            v_bank = ps_v.tile([P, PAIR, KV_COLS], F32, name="v_bank")
+            v_bank = ps_v.tile([P, PAIR, 2 * KV_COLS], F32, name="v_bank")
             members = []
             for a in range(PAIR):
                 one_pass(sums[:, a, :], a, 0, 256, True, False)
@@ -229,7 +229,7 @@ def tile_transformerblock_pa_t_kernel(
                 members.append(bank)
                 one_pass(bank[:, 0:256], a, 0, 256, True, True)
                 one_pass(bank[:, 256 : 2 * HALF], a, 256, 2 * HALF, True, True)
-                one_pass(v_bank[:, a, :], a, V_AT, V_AT + KV_COLS, True, True)
+                one_pass(v_bank[:, a, :], a, V_AT - KV_COLS, V_AT + KV_COLS, True, True)
             banks_of_pair[pair] = (sums, v_bank, members)
 
         def copy_v(pair):
@@ -239,7 +239,7 @@ def tile_transformerblock_pa_t_kernel(
                 k_out = outs.tile([P, GROUP, KV_COLS], F32, name="k_out")
                 v_out = outs.tile([P, GROUP, KV_COLS], F32, name="v_out")
                 outs_of_group[g] = (q_out, k_out, v_out)
-            nc.scalar.copy(out=outs_of_group[g][2][:, first : first + PAIR, :], in_=banks_of_pair[pair][1][:])
+            nc.scalar.copy(out=outs_of_group[g][2][:, first : first + PAIR, :], in_=banks_of_pair[pair][1][:, :, KV_COLS:])
 
         def common_products(pair):
             t0 = pair * PAIR

@@ -89,7 +89,7 @@ def tile_transformerblock_pa_t_kernel(
         ones = const.tile([P, P], BF16)
         nc.vector.memset(ones[:], 1.0)
         warm = const.tile([P, 1], F32)
-        nc.scalar.activation(out=warm[:], in_=eps[:], func=ACT.Sqrt)
+        nc.scalar.activation(out=warm[:], in_=eps[:], func=ACT.Abs_reciprocal_sqrt)
 
         mix = const.tile([P, TILES, ANGLES, 2], F32)
         minus_sin = const.tile([P, TILES, ANGLES], BF16)
@@ -132,7 +132,6 @@ def tile_transformerblock_pa_t_kernel(
         nc.vector.quantize_mx(out=w_codes[:].bitcast(FP8X4), scales=w_scales[:], in_=w_grouped[:])
 
         sums_of_batch = {}
-        std_of_batch = {}
         rstd_of_tile = {}
         turned_of_pair = {}
         codes_of_pair = {}
@@ -160,20 +159,15 @@ def tile_transformerblock_pa_t_kernel(
                     accum_out=sums_of_batch[first][:, t - first : t - first + 1],
                 )
             if (pair + 1) * PAIR == first + count:
-                std = stats.tile([P, GROUP], F32, name="std")
+                rstd = stats.tile([P, GROUP], F32, name="rstd")
                 nc.scalar.activation(
-                    out=std[:, 0:count], in_=sums_of_batch.pop(first)[:, 0:count], func=ACT.Sqrt,
+                    out=rstd[:, 0:count], in_=sums_of_batch.pop(first)[:, 0:count], func=ACT.Abs_reciprocal_sqrt,
                     bias=eps[:], scale=1.0 / DIM,
                 )
-                std_of_batch[first] = std
-
-        def normalise(pair):
-            first, count = batch_of(pair)
-            if pair * PAIR == first:
-                rstd = stats.tile([P, GROUP], F32, name="rstd")
-                nc.vector.reciprocal(out=rstd[:, 0:count], in_=std_of_batch.pop(first)[:, 0:count])
                 for i in range(count):
                     rstd_of_tile[first + i] = rstd[:, i : i + 1]
+
+        def normalise(pair):
             h = work.tile([P, PAIR, DIM], BF16, name="h")
             turned = ps_t.tile([P, PAIR, 2, P], F32, tag="turned")
             for a in range(PAIR):
@@ -281,9 +275,11 @@ def tile_transformerblock_pa_t_kernel(
             common, own = products_of_group[g]
             q_half = Q_COLS // 2
             here = slice(first, first + PAIR)
-            add_products(q_out[:, here, :], own[:, here, 0:Q_COLS], common[:, here, 0:q_half])
+            for at in range(first, first + PAIR):
+                one = slice(at, at + 1)
+                add_products(q_out[:, one, :], own[:, one, 0:Q_COLS], common[:, one, 0:q_half])
+            add_products(k_out[:, here, :], own[:, here, Q_COLS : 2 * HALF], common[:, here, q_half:HALF])
             if first + PAIR == GROUP:
-                add_products(k_out[:], own[:, :, Q_COLS : 2 * HALF], common[:, :, q_half:HALF])
                 tiles = slice(g * GROUP, (g + 1) * GROUP)
                 nc.sync.dma_start(out=v_view[:, tiles, :], in_=v_out[:])
                 nc.sync.dma_start(out=q_view[:, tiles, :], in_=q_out[:])

@@ -30,6 +30,8 @@ N_GROUPS = TILES // GROUP
 
 ODD_Q, ODD_K, EVEN_Q, EVEN_K, V_AT = 0, 128, 192, 320, 384
 W_COLS = 512
+MIX_TILES = 16
+MIX_STEPS = [-2, 1, 3, 5]
 
 FLOPS = 2 * TOKENS * DIM * (Q_COLS + 2 * KV_COLS)
 
@@ -50,7 +52,7 @@ def tile_transformerblock_pa_t_kernel(
     with (
         tc.tile_pool(name="const", bufs=1) as const,
         tc.tile_pool(name="xin", bufs=N_GROUPS) as xin,
-        tc.tile_pool(name="stats", bufs=4) as stats,
+        tc.tile_pool(name="stats", bufs=6) as stats,
         tc.tile_pool(name="work", bufs=3) as work,
         tc.tile_pool(name="outs", bufs=4) as outs,
         tc.psum_pool(name="ps_gain", bufs=1) as ps_gain,
@@ -60,27 +62,27 @@ def tile_transformerblock_pa_t_kernel(
         tc.psum_pool(name="ps_v", bufs=1) as ps_v,
         tc.manual_schedule(),
     ):
+        x_groups = []
+        for g in range(N_GROUPS):
+            x_sb = xin.tile([P, GROUP, DIM], BF16, name="x_sb")
+            x_groups.append(x_sb)
+        gain_row = const.tile([P, DIM], BF16)
+        nc.vector.memset(gain_row[:], 0.0)
+        nc.sync.dma_start(out=gain_row[0:1, :], in_=attn_norm_w.rearrange("(o k) -> o k", o=1))
+        nc.sync.dma_start(out=x_groups[0][:, 0, :], in_=x_view[:, 0, :])
+        nc.sync.dma_start(out=x_groups[0][:, 1, :], in_=x_view[:, 1, :])
         w_raw = const.tile([P, 4, DIM], BF16)
         nc.sync.dma_start(out=w_raw[:, 0:2, :], in_=wq.rearrange("(n e) k -> n e k", e=2))
         nc.sync.dma_start(out=w_raw[0:64, 2, :], in_=wk_view[:, 0, :])
         nc.sync.dma_start(out=w_raw[64:128, 2, :], in_=wk_view[:, 1, :])
         nc.sync.dma_start(out=w_raw[:, 3, :], in_=wv)
-        gain_row = const.tile([P, DIM], BF16)
-        nc.vector.memset(gain_row[:], 0.0)
-        x_groups = []
-        for g in range(N_GROUPS):
-            x_sb = xin.tile([P, GROUP, DIM], BF16, name="x_sb")
-            x_groups.append(x_sb)
-        nc.sync.dma_start(out=x_groups[0][:, 0:PAIR, :], in_=x_view[:, 0:PAIR, :])
-        nc.sync.dma_start(out=gain_row[0:1, :], in_=attn_norm_w.rearrange("(o k) -> o k", o=1))
         nc.sync.dma_start(out=x_groups[0][:, PAIR:GROUP, :], in_=x_view[:, PAIR:GROUP, :])
         cos_sb = const.tile([P, TILES, ANGLES], BF16)
         sin_sb = const.tile([P, TILES, ANGLES], BF16)
+        nc.sync.dma_start(out=cos_sb[:], in_=cos_view)
+        nc.sync.dma_start(out=sin_sb[:], in_=sin_view)
         for g in range(1, N_GROUPS):
             nc.sync.dma_start(out=x_groups[g][:], in_=x_view[:, g * GROUP : (g + 1) * GROUP, :])
-            if g == 1:
-                nc.sync.dma_start(out=cos_sb[:], in_=cos_view)
-                nc.sync.dma_start(out=sin_sb[:], in_=sin_view)
 
         ident = const.tile([P, P], F32)
         make_identity(nc, ident[:])
@@ -88,48 +90,69 @@ def tile_transformerblock_pa_t_kernel(
         nc.vector.memset(eps[:], EPS)
         ones = const.tile([P, P], BF16)
         nc.vector.memset(ones[:], 1.0)
+        plus = const.tile([P, P], BF16)
+        nc.vector.tensor_copy(out=plus[:], in_=ident[:])
+        minus = const.tile([P, P], BF16)
+        nc.vector.tensor_scalar(minus[:], ident[:], -1.0, None, op0=ALU.mult)
         warm = const.tile([P, 1], F32)
         nc.scalar.activation(out=warm[:], in_=eps[:], func=ACT.Abs_reciprocal_sqrt)
+        gain = ps_gain.tile([P, DIM], F32)
+        nc.tensor.matmul(gain[:], lhsT=ones[:], rhs=gain_row[:], start=True, stop=True)
 
         mix = const.tile([P, TILES, ANGLES, 2], F32)
-        minus_sin = const.tile([P, TILES, ANGLES], BF16)
+        bank_of_part = {}
 
-        def build_mix(lo, hi):
-            nc.gpsimd.tensor_scalar(
-                minus_sin[:, lo:hi, :], sin_sb[:, lo:hi, :], -1.0, 0.0, op0=ALU.mult, op1=ALU.add
-            )
-            nc.gpsimd.tensor_tensor(
-                out=mix[:, lo:hi, :, 0], in0=minus_sin[:, lo:hi, :], in1=cos_sb[:, lo:hi, :], op=ALU.subtract
-            )
-            nc.gpsimd.tensor_tensor(
-                out=mix[:, lo:hi, :, 1], in0=sin_sb[:, lo:hi, :], in1=cos_sb[:, lo:hi, :], op=ALU.subtract
+        def add_factors(part):
+            lo, hi = part * MIX_TILES, (part + 1) * MIX_TILES
+            cos_part = cos_sb[:, lo:hi, :].rearrange("p t j -> p (t j)")
+            sin_part = sin_sb[:, lo:hi, :].rearrange("p t j -> p (t j)")
+            bank = ps_eo.tile([P, 512], F32, name="bank")
+            half = MIX_TILES * ANGLES
+            nc.tensor.matmul(bank[:, 0:half], lhsT=minus[:], rhs=cos_part, start=True, stop=False)
+            nc.tensor.matmul(bank[:, 0:half], lhsT=minus[:], rhs=sin_part, start=False, stop=True)
+            nc.tensor.matmul(bank[:, half:], lhsT=minus[:], rhs=cos_part, start=True, stop=False)
+            nc.tensor.matmul(bank[:, half:], lhsT=plus[:], rhs=sin_part, start=False, stop=True)
+            bank_of_part[part] = bank
+
+        def copy_factors(part):
+            lo, hi = part * MIX_TILES, (part + 1) * MIX_TILES
+            bank = bank_of_part.pop(part)
+            nc.scalar.copy(
+                out=mix[:, lo:hi, :, :].rearrange("p t j e -> p (t j) e"),
+                in_=bank[:].rearrange("p (e n) -> p n e", e=2),
             )
 
         w_grouped = const.tile([P, W_COLS * 4], BF16, align_bytes=64)
         w_words = w_grouped[:].bitcast(F32).rearrange("p (n u) -> p n u", u=2)
+        w_codes = const.tile([P, W_COLS], U32, align_bytes=64)
+        w_scales = const.tile([P, W_COLS], U8, align_bytes=64)
         w_places = [
             [(0, P, EVEN_Q)],
             [(0, P, ODD_Q)],
             [(0, 64, EVEN_K), (64, P, ODD_K)],
             [(0, P, V_AT)],
         ]
-        for half in range(2):
-            w_t = ps_t.tile([P, 2, 2, P], F32, tag="turned")
-            for a in range(2):
-                for u in range(2):
-                    nc.tensor.transpose(
-                        w_t[:, a, u, :], w_raw[:, 2 * half + a, :].bitcast(F32)[:, u : 2 * P : 2], ident[:]
-                    )
-            for a in range(2):
-                for lo, hi, at in w_places[2 * half + a]:
+        w_turned = []
+
+        def turn_weights():
+            for half in range(2):
+                bank = ps_eo.tile([P, 512], F32, name="bank")
+                w_t = bank[:].rearrange("p (a u n) -> p a u n", a=2, u=2)
+                w_turned.append(w_t)
+                for a in range(2):
+                    for u in range(2):
+                        nc.tensor.transpose(
+                            w_t[:, a, u, :], w_raw[:, 2 * half + a, :].bitcast(F32)[:, u : 2 * P : 2], ident[:]
+                        )
+
+        def quantise_weights():
+            for block in range(4):
+                for lo, hi, at in w_places[block]:
                     nc.vector.tensor_copy(
-                        out=w_words[:, at : at + hi - lo, :], in_=w_t[:, a, :, lo:hi].rearrange("p u n -> p n u")
+                        out=w_words[:, at : at + hi - lo, :],
+                        in_=w_turned[block // 2][:, block % 2, :, lo:hi].rearrange("p u n -> p n u"),
                     )
-        gain = ps_gain.tile([P, DIM], F32)
-        nc.tensor.matmul(gain[:], lhsT=ones[:], rhs=gain_row[:], start=True, stop=True)
-        w_codes = const.tile([P, W_COLS], U32, align_bytes=64)
-        w_scales = const.tile([P, W_COLS], U8, align_bytes=64)
-        nc.vector.quantize_mx(out=w_codes[:].bitcast(FP8X4), scales=w_scales[:], in_=w_grouped[:])
+            nc.vector.quantize_mx(out=w_codes[:].bitcast(FP8X4), scales=w_scales[:], in_=w_grouped[:])
 
         sums_of_batch = {}
         rstd_of_tile = {}
@@ -140,32 +163,31 @@ def tile_transformerblock_pa_t_kernel(
         outs_of_group = {}
         products_of_group = {}
 
-        def batch_of(pair):
-            t0 = pair * PAIR
-            if t0 < GROUP:
-                return t0, PAIR
-            return t0 - t0 % GROUP, GROUP
+        def batch_of(t):
+            if t < GROUP:
+                return t, 1
+            return t - t % GROUP, GROUP
 
         def squares(pair):
-            first, count = batch_of(pair)
-            if pair * PAIR == first:
-                sumsq = stats.tile([P, GROUP], F32, name="sumsq")
-                sums_of_batch[first] = sumsq
             for t in range(pair * PAIR, (pair + 1) * PAIR):
                 g, at = divmod(t, GROUP)
+                first, count = batch_of(t)
+                if t == first:
+                    sumsq = stats.tile([P, GROUP], F32, name="sumsq")
+                    sums_of_batch[first] = sumsq
                 junk = stats.tile([P, DIM], BF16, name="junk")
                 nc.scalar.activation(
                     out=junk[:], in_=x_groups[g][:, at, :], func=ACT.Square,
                     accum_out=sums_of_batch[first][:, t - first : t - first + 1],
                 )
-            if (pair + 1) * PAIR == first + count:
-                rstd = stats.tile([P, GROUP], F32, name="rstd")
-                nc.scalar.activation(
-                    out=rstd[:, 0:count], in_=sums_of_batch.pop(first)[:, 0:count], func=ACT.Abs_reciprocal_sqrt,
-                    bias=eps[:], scale=1.0 / DIM,
-                )
-                for i in range(count):
-                    rstd_of_tile[first + i] = rstd[:, i : i + 1]
+                if t + 1 == first + count:
+                    rstd = stats.tile([P, GROUP], F32, name="rstd")
+                    nc.scalar.activation(
+                        out=rstd[:, 0:count], in_=sums_of_batch.pop(first)[:, 0:count],
+                        func=ACT.Abs_reciprocal_sqrt, bias=eps[:], scale=1.0 / DIM,
+                    )
+                    for i in range(count):
+                        rstd_of_tile[first + i] = rstd[:, i : i + 1]
 
         def normalise(pair):
             h = work.tile([P, PAIR, DIM], BF16, name="h")
@@ -260,9 +282,9 @@ def tile_transformerblock_pa_t_kernel(
                 op=ALU.mult,
             )
 
-        def add_products(out, own, common):
+        def add_products(engine, out, own, common):
             tiles, pairs = common.shape[1], common.shape[2]
-            nc.gpsimd.tensor_tensor(
+            engine.tensor_tensor(
                 out=out.rearrange("p a (n e) -> p a n e", e=2),
                 in0=own.rearrange("p a (n e) -> p a n e", e=2),
                 in1=common.unsqueeze(3).to_broadcast([P, tiles, pairs, 2]),
@@ -275,11 +297,19 @@ def tile_transformerblock_pa_t_kernel(
             common, own = products_of_group[g]
             q_half = Q_COLS // 2
             here = slice(first, first + PAIR)
+            last = pair == N_PAIRS - 1
             for at in range(first, first + PAIR):
+                engine = nc.vector if last and at == first + PAIR - 1 else nc.gpsimd
                 one = slice(at, at + 1)
-                add_products(q_out[:, one, :], own[:, one, 0:Q_COLS], common[:, one, 0:q_half])
-            add_products(k_out[:, here, :], own[:, here, Q_COLS : 2 * HALF], common[:, here, q_half:HALF])
-            if first + PAIR == GROUP:
+                add_products(engine, q_out[:, one, :], own[:, one, 0:Q_COLS], common[:, one, 0:q_half])
+            engine = nc.vector if last else nc.gpsimd
+            add_products(engine, k_out[:, here, :], own[:, here, Q_COLS : 2 * HALF], common[:, here, q_half:HALF])
+            if g == N_GROUPS - 1:
+                tiles = slice(pair * PAIR, (pair + 1) * PAIR)
+                nc.sync.dma_start(out=v_view[:, tiles, :], in_=v_out[:, here, :])
+                nc.sync.dma_start(out=q_view[:, tiles, :], in_=q_out[:, here, :])
+                nc.sync.dma_start(out=k_view[:, tiles, :], in_=k_out[:, here, :])
+            elif first + PAIR == GROUP:
                 tiles = slice(g * GROUP, (g + 1) * GROUP)
                 nc.sync.dma_start(out=v_view[:, tiles, :], in_=v_out[:])
                 nc.sync.dma_start(out=q_view[:, tiles, :], in_=q_out[:])
@@ -290,18 +320,29 @@ def tile_transformerblock_pa_t_kernel(
 
         for s in range(-5, N_PAIRS):
             if s == -3:
-                build_mix(0, 16)
-            elif s == -1:
-                build_mix(16, TILES)
+                turn_weights()
+            if s < 0:
+                on(words, s + 2)
             on(copy_v, s)
-            on(common_products, s)
-            if 0 <= s:
+            if s - 1 in MIX_STEPS:
+                copy_factors(MIX_STEPS.index(s - 1))
+            if s + 3 < N_PAIRS:
+                on(common_products, s)
+                own_products(s * PAIR) if 0 <= s else None
+                on(quantise, s + 1)
+            else:
+                on(quantise, s + 1)
+                on(common_products, s)
                 own_products(s * PAIR)
-            on(quantise, s + 1)
             if 0 <= s:
                 own_products(s * PAIR + 1)
             on(project, s + 1)
             on(squares, s + 5)
-            on(words, s + 2)
+            if 0 <= s:
+                on(words, s + 2)
             on(normalise, s + 3)
+            if s == -3:
+                quantise_weights()
+            if s in MIX_STEPS:
+                add_factors(MIX_STEPS.index(s))
             on(add_and_store, s)

@@ -168,8 +168,9 @@ def tile_transformerblock_pa_t_kernel(
                 return t, 1
             return t - t % GROUP, GROUP
 
-        def squares(pair):
-            for t in range(pair * PAIR, (pair + 1) * PAIR):
+        def squares(pair, members=range(PAIR)):
+            for a in members:
+                t = pair * PAIR + a
                 g, at = divmod(t, GROUP)
                 first, count = batch_of(t)
                 if t == first:
@@ -251,11 +252,10 @@ def tile_transformerblock_pa_t_kernel(
         def copy_v(pair):
             g, first = divmod(pair * PAIR, GROUP)
             if first == 0:
-                q_out = outs.tile([P, GROUP, Q_COLS], F32, name="q_out")
-                k_out = outs.tile([P, GROUP, KV_COLS], F32, name="k_out")
+                turned_out = outs.tile([P, GROUP, 2 * HALF], F32, name="turned_out")
                 v_out = outs.tile([P, GROUP, KV_COLS], F32, name="v_out")
-                outs_of_group[g] = (q_out, k_out, v_out)
-            nc.scalar.copy(out=outs_of_group[g][2][:, first : first + PAIR, :], in_=banks_of_pair[pair][1][:, :, KV_COLS:])
+                outs_of_group[g] = (turned_out, v_out)
+            nc.scalar.copy(out=outs_of_group[g][1][:, first : first + PAIR, :], in_=banks_of_pair[pair][1][:, :, KV_COLS:])
 
         def common_products(pair):
             t0 = pair * PAIR
@@ -282,38 +282,33 @@ def tile_transformerblock_pa_t_kernel(
                 op=ALU.mult,
             )
 
-        def add_products(engine, out, own, common):
-            tiles, pairs = common.shape[1], common.shape[2]
+        def add_products(tile):
+            g, at = divmod(tile, GROUP)
+            common, own = products_of_group[g]
+            engine = nc.vector if tile == TILES - 1 else nc.gpsimd
             engine.tensor_tensor(
-                out=out.rearrange("p a (n e) -> p a n e", e=2),
-                in0=own.rearrange("p a (n e) -> p a n e", e=2),
-                in1=common.unsqueeze(3).to_broadcast([P, tiles, pairs, 2]),
+                out=outs_of_group[g][0][:, at, :].rearrange("p (n e) -> p n e", e=2),
+                in0=own[:, at, :].rearrange("p (n e) -> p n e", e=2),
+                in1=common[:, at, :].unsqueeze(2).to_broadcast([P, HALF, 2]),
                 op=ALU.add,
             )
 
+        def store(first_tile, count):
+            g, at = divmod(first_tile, GROUP)
+            turned_out, v_out = outs_of_group[g]
+            tiles, here = slice(first_tile, first_tile + count), slice(at, at + count)
+            nc.sync.dma_start(out=v_view[:, tiles, :], in_=v_out[:, here, :])
+            nc.sync.dma_start(out=q_view[:, tiles, :], in_=turned_out[:, here, 0:Q_COLS])
+            nc.sync.dma_start(out=k_view[:, tiles, :], in_=turned_out[:, here, Q_COLS:])
+
         def add_and_store(pair):
-            g, first = divmod(pair * PAIR, GROUP)
-            q_out, k_out, v_out = outs_of_group[g]
-            common, own = products_of_group[g]
-            q_half = Q_COLS // 2
-            here = slice(first, first + PAIR)
-            last = pair == N_PAIRS - 1
-            for at in range(first, first + PAIR):
-                engine = nc.vector if last and at == first + PAIR - 1 else nc.gpsimd
-                one = slice(at, at + 1)
-                add_products(engine, q_out[:, one, :], own[:, one, 0:Q_COLS], common[:, one, 0:q_half])
-            engine = nc.vector if last else nc.gpsimd
-            add_products(engine, k_out[:, here, :], own[:, here, Q_COLS : 2 * HALF], common[:, here, q_half:HALF])
-            if g == N_GROUPS - 1:
-                tiles = slice(pair * PAIR, (pair + 1) * PAIR)
-                nc.sync.dma_start(out=v_view[:, tiles, :], in_=v_out[:, here, :])
-                nc.sync.dma_start(out=q_view[:, tiles, :], in_=q_out[:, here, :])
-                nc.sync.dma_start(out=k_view[:, tiles, :], in_=k_out[:, here, :])
-            elif first + PAIR == GROUP:
-                tiles = slice(g * GROUP, (g + 1) * GROUP)
-                nc.sync.dma_start(out=v_view[:, tiles, :], in_=v_out[:])
-                nc.sync.dma_start(out=q_view[:, tiles, :], in_=q_out[:])
-                nc.sync.dma_start(out=k_view[:, tiles, :], in_=k_out[:])
+            for tile in range(pair * PAIR, (pair + 1) * PAIR):
+                add_products(tile)
+            t0 = pair * PAIR
+            if t0 >= TILES - GROUP:
+                store(t0, PAIR)
+            elif (t0 + PAIR) % GROUP == 0:
+                store(t0 + PAIR - GROUP, GROUP)
 
         def on(stage, pair):
             return stage(pair) if 0 <= pair < N_PAIRS else None
@@ -337,9 +332,14 @@ def tile_transformerblock_pa_t_kernel(
             if 0 <= s:
                 own_products(s * PAIR + 1)
             on(project, s + 1)
-            on(squares, s + 5)
-            if 0 <= s:
+            if s < 0:
+                on(squares, s + 5)
+            else:
+                if s + 5 < N_PAIRS:
+                    squares(s + 5, [0])
                 on(words, s + 2)
+                if s + 5 < N_PAIRS:
+                    squares(s + 5, [1])
             on(normalise, s + 3)
             if s == -3:
                 quantise_weights()

@@ -31,7 +31,7 @@ N_GROUPS = TILES // GROUP
 ODD_Q, ODD_K, EVEN_Q, EVEN_K, V_AT = 0, 128, 192, 320, 384
 W_COLS = 512
 MIX_TILES = 16
-MIX_STEPS = [-2, 1, 3, 5]
+FACTOR_STEPS = [1, 3, 5]
 
 FLOPS = 2 * TOKENS * DIM * (Q_COLS + 2 * KV_COLS)
 
@@ -67,9 +67,9 @@ def tile_transformerblock_pa_t_kernel(
             x_sb = xin.tile([P, GROUP, DIM], BF16, name="x_sb")
             x_groups.append(x_sb)
         gain_row = const.tile([P, DIM], BF16)
-        nc.vector.memset(gain_row[:], 0.0)
-        nc.sync.dma_start(out=gain_row[0:1, :], in_=attn_norm_w.rearrange("(o k) -> o k", o=1))
+        nc.vector.memset(gain_row[:].bitcast(F32), 0.0)
         nc.sync.dma_start(out=x_groups[0][:, 0, :], in_=x_view[:, 0, :])
+        nc.sync.dma_start(out=gain_row[0:1, :], in_=attn_norm_w.rearrange("(o k) -> o k", o=1))
         nc.sync.dma_start(out=x_groups[0][:, 1, :], in_=x_view[:, 1, :])
         w_raw = const.tile([P, 4, DIM], BF16)
         nc.sync.dma_start(out=w_raw[:, 0:2, :], in_=wq.rearrange("(n e) k -> n e k", e=2))
@@ -164,9 +164,8 @@ def tile_transformerblock_pa_t_kernel(
         products_of_group = {}
 
         def batch_of(t):
-            if t < GROUP:
-                return t, 1
-            return t - t % GROUP, GROUP
+            count = 1 if t < GROUP else PAIR if t < 2 * GROUP else GROUP
+            return t - t % count, count
 
         def squares(pair, members=range(PAIR)):
             for a in members:
@@ -305,44 +304,52 @@ def tile_transformerblock_pa_t_kernel(
             for tile in range(pair * PAIR, (pair + 1) * PAIR):
                 add_products(tile)
             t0 = pair * PAIR
-            if t0 >= TILES - GROUP:
+            if pair == N_PAIRS - 1:
+                for tile in range(t0, t0 + PAIR):
+                    store(tile, 1)
+            elif pair == N_PAIRS - 2:
                 store(t0, PAIR)
             elif (t0 + PAIR) % GROUP == 0:
                 store(t0 + PAIR - GROUP, GROUP)
 
-        def on(stage, pair):
-            return stage(pair) if 0 <= pair < N_PAIRS else None
+        def on(stage, pair, *more):
+            if 0 <= pair < N_PAIRS:
+                stage(pair, *more)
 
-        for s in range(-5, N_PAIRS):
-            if s == -3:
-                turn_weights()
-            if s < 0:
-                on(words, s + 2)
-            on(copy_v, s)
-            if s - 1 in MIX_STEPS:
-                copy_factors(MIX_STEPS.index(s - 1))
+        squares(0)
+        squares(1)
+        turn_weights()
+        normalise(0)
+        words(0)
+        squares(2)
+        add_factors(0)
+        copy_factors(0)
+        quantise_weights()
+        quantise(0)
+        project(0)
+        normalise(1)
+        squares(3)
+        words(1)
+        normalise(2)
+        squares(4)
+        for s in range(N_PAIRS):
+            copy_v(s)
+            if s - 1 in FACTOR_STEPS:
+                copy_factors(1 + FACTOR_STEPS.index(s - 1))
             if s + 3 < N_PAIRS:
-                on(common_products, s)
-                own_products(s * PAIR) if 0 <= s else None
-                on(quantise, s + 1)
-            else:
-                on(quantise, s + 1)
-                on(common_products, s)
+                common_products(s)
                 own_products(s * PAIR)
-            if 0 <= s:
-                own_products(s * PAIR + 1)
-            on(project, s + 1)
-            if s < 0:
-                on(squares, s + 5)
+                on(quantise, s + 1)
             else:
-                if s + 5 < N_PAIRS:
-                    squares(s + 5, [0])
-                on(words, s + 2)
-                if s + 5 < N_PAIRS:
-                    squares(s + 5, [1])
+                on(quantise, s + 1)
+                common_products(s)
+                own_products(s * PAIR)
+            own_products(s * PAIR + 1)
+            on(project, s + 1)
+            on(squares, s + 5, [0])
+            on(words, s + 2)
+            on(squares, s + 5, [1])
             on(normalise, s + 3)
-            if s == -3:
-                quantise_weights()
-            if s in MIX_STEPS:
-                add_factors(MIX_STEPS.index(s))
-            on(add_and_store, s)
+            if s in FACTOR_STEPS:
+                add_factors(1 + FACTOR_STEPS.index(s))
+            add_and_store(s)

@@ -31,7 +31,7 @@ N_GROUPS = TILES // GROUP
 ODD_Q, ODD_K, EVEN_Q, EVEN_K, V_AT = 0, 128, 192, 320, 384
 W_COLS = 512
 MIX_TILES = 16
-FACTOR_STEPS = [1, 3, 5]
+FACTOR_STEPS = [2, 4, 6]
 
 FLOPS = 2 * TOKENS * DIM * (Q_COLS + 2 * KV_COLS)
 
@@ -67,9 +67,9 @@ def tile_transformerblock_pa_t_kernel(
             x_sb = xin.tile([P, GROUP, DIM], BF16, name="x_sb")
             x_groups.append(x_sb)
         gain_row = const.tile([P, DIM], BF16)
-        nc.vector.memset(gain_row[:].bitcast(F32), 0.0)
-        nc.sync.dma_start(out=x_groups[0][:, 0, :], in_=x_view[:, 0, :])
+        nc.gpsimd.memset(gain_row[:].bitcast(F32), 0.0)
         nc.sync.dma_start(out=gain_row[0:1, :], in_=attn_norm_w.rearrange("(o k) -> o k", o=1))
+        nc.sync.dma_start(out=x_groups[0][:, 0, :], in_=x_view[:, 0, :])
         nc.sync.dma_start(out=x_groups[0][:, 1, :], in_=x_view[:, 1, :])
         w_raw = const.tile([P, 4, DIM], BF16)
         nc.sync.dma_start(out=w_raw[:, 0:2, :], in_=wq.rearrange("(n e) k -> n e k", e=2))
@@ -281,10 +281,13 @@ def tile_transformerblock_pa_t_kernel(
                 op=ALU.mult,
             )
 
+        def is_late(pair):
+            return pair + 3 >= N_PAIRS
+
         def add_products(tile):
             g, at = divmod(tile, GROUP)
             common, own = products_of_group[g]
-            engine = nc.vector if tile == TILES - 1 else nc.gpsimd
+            engine = nc.vector if is_late(tile // PAIR) and tile % PAIR == 1 else nc.gpsimd
             engine.tensor_tensor(
                 out=outs_of_group[g][0][:, at, :].rearrange("p (n e) -> p n e", e=2),
                 in0=own[:, at, :].rearrange("p (n e) -> p n e", e=2),
@@ -292,25 +295,34 @@ def tile_transformerblock_pa_t_kernel(
                 op=ALU.add,
             )
 
-        def store(first_tile, count):
+        def store_v(first_tile, count):
             g, at = divmod(first_tile, GROUP)
-            turned_out, v_out = outs_of_group[g]
+            tiles = slice(first_tile, first_tile + count)
+            nc.sync.dma_start(out=v_view[:, tiles, :], in_=outs_of_group[g][1][:, at : at + count, :])
+
+        def store_q_and_k(first_tile, count):
+            g, at = divmod(first_tile, GROUP)
             tiles, here = slice(first_tile, first_tile + count), slice(at, at + count)
-            nc.sync.dma_start(out=v_view[:, tiles, :], in_=v_out[:, here, :])
+            turned_out = outs_of_group[g][0]
             nc.sync.dma_start(out=q_view[:, tiles, :], in_=turned_out[:, here, 0:Q_COLS])
             nc.sync.dma_start(out=k_view[:, tiles, :], in_=turned_out[:, here, Q_COLS:])
 
-        def add_and_store(pair):
-            for tile in range(pair * PAIR, (pair + 1) * PAIR):
-                add_products(tile)
+        def add_and_store(pair, members=range(PAIR)):
             t0 = pair * PAIR
+            for a in members:
+                add_products(t0 + a)
+            done = t0 + members[-1] + 1
             if pair == N_PAIRS - 1:
-                for tile in range(t0, t0 + PAIR):
-                    store(tile, 1)
+                if done < TILES:
+                    store_v(t0, PAIR)
+                store_q_and_k(done - 1, 1)
             elif pair == N_PAIRS - 2:
-                store(t0, PAIR)
-            elif (t0 + PAIR) % GROUP == 0:
-                store(t0 + PAIR - GROUP, GROUP)
+                if done % PAIR == 0:
+                    store_v(t0, PAIR)
+                    store_q_and_k(t0, PAIR)
+            elif done % GROUP == 0:
+                store_v(done - GROUP, GROUP)
+                store_q_and_k(done - GROUP, GROUP)
 
         def on(stage, pair, *more):
             if 0 <= pair < N_PAIRS:
@@ -334,22 +346,23 @@ def tile_transformerblock_pa_t_kernel(
         squares(4)
         for s in range(N_PAIRS):
             copy_v(s)
-            if s - 1 in FACTOR_STEPS:
-                copy_factors(1 + FACTOR_STEPS.index(s - 1))
+            if s + 3 >= N_PAIRS:
+                on(quantise, s + 1)
+            common_products(s)
+            own_products(s * PAIR)
             if s + 3 < N_PAIRS:
-                common_products(s)
-                own_products(s * PAIR)
                 on(quantise, s + 1)
-            else:
-                on(quantise, s + 1)
-                common_products(s)
-                own_products(s * PAIR)
+            if is_late(s - 1):
+                add_and_store(s - 1, [1])
             own_products(s * PAIR + 1)
             on(project, s + 1)
             on(squares, s + 5, [0])
             on(words, s + 2)
+            if s - 1 in FACTOR_STEPS:
+                copy_factors(1 + FACTOR_STEPS.index(s - 1))
             on(squares, s + 5, [1])
             on(normalise, s + 3)
             if s in FACTOR_STEPS:
                 add_factors(1 + FACTOR_STEPS.index(s))
-            add_and_store(s)
+            add_and_store(s, [0] if is_late(s) else range(PAIR))
+        add_and_store(N_PAIRS - 1, [1])

@@ -31,6 +31,7 @@ N_GROUPS = TILES // GROUP
 ODD_Q, ODD_K, EVEN_Q, EVEN_K, V_AT = 0, 128, 192, 320, 384
 W_COLS = 512
 MIX_TILES = 16
+SCALAR_TILES = [17, 29, 41, 53]
 FACTOR_STEPS = [2, 4, 6]
 
 FLOPS = 2 * TOKENS * DIM * (Q_COLS + 2 * KV_COLS)
@@ -52,6 +53,7 @@ def tile_transformerblock_pa_t_kernel(
     with (
         tc.tile_pool(name="const", bufs=1) as const,
         tc.tile_pool(name="xin", bufs=N_GROUPS) as xin,
+        tc.tile_pool(name="xearly", bufs=len(SCALAR_TILES)) as xearly,
         tc.tile_pool(name="stats", bufs=6) as stats,
         tc.tile_pool(name="work", bufs=3) as work,
         tc.tile_pool(name="outs", bufs=4) as outs,
@@ -71,18 +73,32 @@ def tile_transformerblock_pa_t_kernel(
         nc.sync.dma_start(out=gain_row[0:1, :], in_=attn_norm_w.rearrange("(o k) -> o k", o=1))
         nc.sync.dma_start(out=x_groups[0][:, 0, :], in_=x_view[:, 0, :])
         nc.sync.dma_start(out=x_groups[0][:, 1, :], in_=x_view[:, 1, :])
+        early = {}
+        for t in SCALAR_TILES:
+            x_early = xearly.tile([P, DIM], BF16, name="x_early")
+            early[t] = x_early
+
+        def load_early(i):
+            t = SCALAR_TILES[i]
+            nc.sync.dma_start(out=early[t][:], in_=x_view[:, t, :])
+
         w_raw = const.tile([P, 4, DIM], BF16)
         nc.sync.dma_start(out=w_raw[:, 0:2, :], in_=wq.rearrange("(n e) k -> n e k", e=2))
         nc.sync.dma_start(out=w_raw[0:64, 2, :], in_=wk_view[:, 0, :])
         nc.sync.dma_start(out=w_raw[64:128, 2, :], in_=wk_view[:, 1, :])
         nc.sync.dma_start(out=w_raw[:, 3, :], in_=wv)
         nc.sync.dma_start(out=x_groups[0][:, PAIR:GROUP, :], in_=x_view[:, PAIR:GROUP, :])
+        load_early(0)
         cos_sb = const.tile([P, TILES, ANGLES], BF16)
         sin_sb = const.tile([P, TILES, ANGLES], BF16)
         nc.sync.dma_start(out=cos_sb[:], in_=cos_view)
         nc.sync.dma_start(out=sin_sb[:], in_=sin_view)
+        load_early(1)
         for g in range(1, N_GROUPS):
             nc.sync.dma_start(out=x_groups[g][:], in_=x_view[:, g * GROUP : (g + 1) * GROUP, :])
+            if g == 1:
+                load_early(2)
+                load_early(3)
 
         ident = const.tile([P, P], F32)
         make_identity(nc, ident[:])
@@ -98,6 +114,13 @@ def tile_transformerblock_pa_t_kernel(
         nc.scalar.activation(out=warm[:], in_=eps[:], func=ACT.Abs_reciprocal_sqrt)
         gain = ps_gain.tile([P, DIM], F32)
         nc.tensor.matmul(gain[:], lhsT=ones[:], rhs=gain_row[:], start=True, stop=True)
+        gain_sb = const.tile([P, DIM], BF16)
+        nc.vector.tensor_copy(out=gain_sb[:], in_=gain[:])
+        scaled = {}
+        for t in SCALAR_TILES:
+            x_gain = xearly.tile([P, DIM], F32, name="x_gain")
+            nc.gpsimd.tensor_tensor(out=x_gain[:], in0=early[t][:], in1=gain_sb[:], op=ALU.mult)
+            scaled[t] = x_gain
 
         mix = const.tile([P, TILES, ANGLES, 2], F32)
         bank_of_part = {}
@@ -195,10 +218,14 @@ def tile_transformerblock_pa_t_kernel(
             for a in range(PAIR):
                 t = pair * PAIR + a
                 g, at = divmod(t, GROUP)
-                nc.vector.scalar_tensor_tensor(
-                    out=h[:, a, :], in0=x_groups[g][:, at, :], scalar=rstd_of_tile.pop(t), in1=gain[:],
-                    op0=ALU.mult, op1=ALU.mult,
-                )
+                rstd = rstd_of_tile.pop(t)
+                if t in scaled:
+                    nc.scalar.activation(out=h[:, a, :], in_=scaled[t][:], func=ACT.Copy, scale=rstd)
+                else:
+                    nc.vector.scalar_tensor_tensor(
+                        out=h[:, a, :], in0=x_groups[g][:, at, :], scalar=rstd, in1=gain[:],
+                        op0=ALU.mult, op1=ALU.mult,
+                    )
                 for u in range(2):
                     nc.tensor.transpose(
                         turned[:, a, u, :], h[:, a, :].bitcast(F32)[:, u : 2 * P : 2], ident[:]

@@ -28,10 +28,11 @@ GROUP = 4
 N_PAIRS = TILES // PAIR
 N_GROUPS = TILES // GROUP
 
-ODD_Q, ODD_K, EVEN_Q, EVEN_K, V_AT = 0, 128, 192, 320, 384
+V_AT = 2 * HALF
 W_COLS = 512
 MIX_TILES = 16
-SCALAR_TILES = [17, 29, 41, 53]
+SCALAR_TILES = [19, 31, 43, 55]
+SCALAR_PAIRS = [t // PAIR for t in SCALAR_TILES]
 FACTOR_STEPS = [2, 4, 6]
 
 FLOPS = 2 * TOKENS * DIM * (Q_COLS + 2 * KV_COLS)
@@ -48,6 +49,7 @@ def tile_transformerblock_pa_t_kernel(
     q_view = out_0.rearrange("(p t) h d -> p t (h d)", t=TILES)
     k_view = out_1.rearrange("(p t) h d -> p t (h d)", t=TILES)
     v_view = out_2.rearrange("(p t) h d -> p t (h d)", t=TILES)
+    wq_view = wq.rearrange("(n e) k -> n e k", e=2)
     wk_view = wk.rearrange("(n e) k -> n e k", e=2)
 
     with (
@@ -55,7 +57,7 @@ def tile_transformerblock_pa_t_kernel(
         tc.tile_pool(name="xin", bufs=N_GROUPS) as xin,
         tc.tile_pool(name="xearly", bufs=len(SCALAR_TILES)) as xearly,
         tc.tile_pool(name="stats", bufs=6) as stats,
-        tc.tile_pool(name="work", bufs=3) as work,
+        tc.tile_pool(name="work", bufs=4) as work,
         tc.tile_pool(name="outs", bufs=4) as outs,
         tc.psum_pool(name="ps_gain", bufs=1) as ps_gain,
         tc.psum_pool(name="ps_t", bufs=2) as ps_t,
@@ -82,23 +84,25 @@ def tile_transformerblock_pa_t_kernel(
             t = SCALAR_TILES[i]
             nc.sync.dma_start(out=early[t][:], in_=x_view[:, t, :])
 
-        w_raw = const.tile([P, 4, DIM], BF16)
-        nc.sync.dma_start(out=w_raw[:, 0:2, :], in_=wq.rearrange("(n e) k -> n e k", e=2))
-        nc.sync.dma_start(out=w_raw[0:64, 2, :], in_=wk_view[:, 0, :])
-        nc.sync.dma_start(out=w_raw[64:128, 2, :], in_=wk_view[:, 1, :])
-        nc.sync.dma_start(out=w_raw[:, 3, :], in_=wv)
-        nc.sync.dma_start(out=x_groups[0][:, PAIR:GROUP, :], in_=x_view[:, PAIR:GROUP, :])
         load_early(0)
+        w_raw = const.tile([P, 4, DIM], BF16)
+        nc.sync.dma_start(out=w_raw[:, 0, :], in_=wq_view[:, 1, :])
+        nc.sync.dma_start(out=w_raw[:, 1, :], in_=wq_view[:, 0, :])
+        nc.sync.dma_start(out=x_groups[0][:, PAIR:GROUP, :], in_=x_view[:, PAIR:GROUP, :])
+        nc.sync.dma_start(out=w_raw[0:64, 2, :], in_=wk_view[:, 1, :])
+        nc.sync.dma_start(out=w_raw[64:128, 2, :], in_=wk_view[:, 0, :])
+        nc.sync.dma_start(out=w_raw[:, 3, :], in_=wv)
+        load_early(1)
+        nc.sync.dma_start(out=x_groups[1][:, 0:PAIR, :], in_=x_view[:, GROUP : GROUP + PAIR, :])
         cos_sb = const.tile([P, TILES, ANGLES], BF16)
         sin_sb = const.tile([P, TILES, ANGLES], BF16)
         nc.sync.dma_start(out=cos_sb[:], in_=cos_view)
         nc.sync.dma_start(out=sin_sb[:], in_=sin_view)
-        load_early(1)
-        for g in range(1, N_GROUPS):
+        nc.sync.dma_start(out=x_groups[1][:, PAIR:GROUP, :], in_=x_view[:, GROUP + PAIR : 2 * GROUP, :])
+        load_early(2)
+        load_early(3)
+        for g in range(2, N_GROUPS):
             nc.sync.dma_start(out=x_groups[g][:], in_=x_view[:, g * GROUP : (g + 1) * GROUP, :])
-            if g == 1:
-                load_early(2)
-                load_early(3)
 
         ident = const.tile([P, P], F32)
         make_identity(nc, ident[:])
@@ -149,12 +153,6 @@ def tile_transformerblock_pa_t_kernel(
         w_words = w_grouped[:].bitcast(F32).rearrange("p (n u) -> p n u", u=2)
         w_codes = const.tile([P, W_COLS], U32, align_bytes=64)
         w_scales = const.tile([P, W_COLS], U8, align_bytes=64)
-        w_places = [
-            [(0, P, EVEN_Q)],
-            [(0, P, ODD_Q)],
-            [(0, 64, EVEN_K), (64, P, ODD_K)],
-            [(0, P, V_AT)],
-        ]
         w_turned = []
 
         def turn_weights():
@@ -169,16 +167,19 @@ def tile_transformerblock_pa_t_kernel(
                         )
 
         def quantise_weights():
-            for block in range(4):
-                for lo, hi, at in w_places[block]:
-                    nc.vector.tensor_copy(
-                        out=w_words[:, at : at + hi - lo, :],
-                        in_=w_turned[block // 2][:, block % 2, :, lo:hi].rearrange("p u n -> p n u"),
-                    )
+            rope = w_words[:, 0:V_AT, :].rearrange("p (a n) u -> p a n u", a=2)
+            nc.vector.tensor_copy(out=rope[:, :, 0:P, :], in_=w_turned[0].rearrange("p a u n -> p a n u"))
+            nc.vector.tensor_copy(
+                out=rope[:, :, P:HALF, :], in_=w_turned[1][:, 0, :, :].rearrange("p u (a n) -> p a n u", a=2)
+            )
+            nc.vector.tensor_copy(
+                out=w_words[:, V_AT:, :], in_=w_turned[1][:, 1, :, :].rearrange("p u n -> p n u")
+            )
             nc.vector.quantize_mx(out=w_codes[:].bitcast(FP8X4), scales=w_scales[:], in_=w_grouped[:])
 
         sums_of_batch = {}
         rstd_of_tile = {}
+        normed_of_pair = {}
         turned_of_pair = {}
         codes_of_pair = {}
         h_of_pair = {}
@@ -212,18 +213,27 @@ def tile_transformerblock_pa_t_kernel(
                     for i in range(count):
                         rstd_of_tile[first + i] = rstd[:, i : i + 1]
 
-        def normalise(pair):
+        def normalise_on_scalar(pair):
             h = work.tile([P, PAIR, DIM], BF16, name="h")
+            for a in range(PAIR):
+                t = pair * PAIR + a
+                if t in scaled:
+                    nc.scalar.activation(
+                        out=h[:, a, :], in_=scaled[t][:], func=ACT.Copy, scale=rstd_of_tile.pop(t)
+                    )
+            normed_of_pair[pair] = h
+
+        def normalise(pair):
+            if pair not in normed_of_pair:
+                normalise_on_scalar(pair)
+            h = normed_of_pair.pop(pair)
             turned = ps_t.tile([P, PAIR, 2, P], F32, tag="turned")
             for a in range(PAIR):
                 t = pair * PAIR + a
                 g, at = divmod(t, GROUP)
-                rstd = rstd_of_tile.pop(t)
-                if t in scaled:
-                    nc.scalar.activation(out=h[:, a, :], in_=scaled[t][:], func=ACT.Copy, scale=rstd)
-                else:
+                if t not in scaled:
                     nc.vector.scalar_tensor_tensor(
-                        out=h[:, a, :], in0=x_groups[g][:, at, :], scalar=rstd, in1=gain[:],
+                        out=h[:, a, :], in0=x_groups[g][:, at, :], scalar=rstd_of_tile.pop(t), in1=gain[:],
                         op0=ALU.mult, op1=ALU.mult,
                     )
                 for u in range(2):
@@ -389,6 +399,8 @@ def tile_transformerblock_pa_t_kernel(
                 copy_factors(1 + FACTOR_STEPS.index(s - 1))
             on(squares, s + 5, [1])
             on(normalise, s + 3)
+            if s + 4 in SCALAR_PAIRS:
+                normalise_on_scalar(s + 4)
             if s in FACTOR_STEPS:
                 add_factors(1 + FACTOR_STEPS.index(s))
             add_and_store(s, [0] if is_late(s) else range(PAIR))

import concourse.mybir as mybir
from concourse.masks import make_identity

F32 = mybir.dt.float32
BF16 = mybir.dt.bfloat16
U32 = mybir.dt.uint32
U8 = mybir.dt.uint8
FP8X4 = mybir.dt.float8_e4m3fn_x4
ACT = mybir.ActivationFunctionType
ALU = mybir.AluOpType

P = 128
TOKENS = 8192
DIM = 512
HEAD = 32
ANGLES = HEAD // 2
Q_HEADS = 8
K_HEADS = 4
HEADS = Q_HEADS + K_HEADS
Q_COLS = Q_HEADS * HEAD
KV_COLS = K_HEADS * HEAD
HALF = HEADS * ANGLES
EPS = 1e-6

TILES = TOKENS // P
PAIR = 2
GROUP = 4
N_PAIRS = TILES // PAIR
N_GROUPS = TILES // GROUP

V_AT = 2 * HALF
W_COLS = 512
MIX_TILES = 16
SCALAR_TILES = [19, 31, 43, 55]
SCALAR_PAIRS = [t // PAIR for t in SCALAR_TILES]
FACTOR_STEPS = [2, 4, 6]

FLOPS = 2 * TOKENS * DIM * (Q_COLS + 2 * KV_COLS)


def tile_transformerblock_pa_t_kernel(
    tc, x, freqs_cos, freqs_sin, wq, wk, wv, attn_norm_w, out_0, out_1, out_2
):
    nc = tc.nc

    x_view = x.rearrange("(p t) k -> p t k", t=TILES)
    cos_view = freqs_cos.rearrange("(p t) j -> p t j", t=TILES)
    sin_view = freqs_sin.rearrange("(p t) j -> p t j", t=TILES)
    q_view = out_0.rearrange("(p t) h d -> p t (h d)", t=TILES)
    k_view = out_1.rearrange("(p t) h d -> p t (h d)", t=TILES)
    v_view = out_2.rearrange("(p t) h d -> p t (h d)", t=TILES)
    wq_view = wq.rearrange("(n e) k -> n e k", e=2)
    wk_view = wk.rearrange("(n e) k -> n e k", e=2)

    with (
        tc.tile_pool(name="const", bufs=1) as const,
        tc.tile_pool(name="xin", bufs=N_GROUPS) as xin,
        tc.tile_pool(name="xearly", bufs=len(SCALAR_TILES)) as xearly,
        tc.tile_pool(name="stats", bufs=6) as stats,
        tc.tile_pool(name="work", bufs=4) as work,
        tc.tile_pool(name="outs", bufs=4) as outs,
        tc.psum_pool(name="ps_gain", bufs=1) as ps_gain,
        tc.psum_pool(name="ps_t", bufs=2) as ps_t,
        tc.psum_pool(name="ps_eo", bufs=3) as ps_eo,
        tc.psum_pool(name="ps_sum", bufs=1) as ps_sum,
        tc.psum_pool(name="ps_v", bufs=1) as ps_v,
        tc.manual_schedule(),
    ):
        x_groups = []
        for g in range(N_GROUPS):
            x_sb = xin.tile([P, GROUP, DIM], BF16, name="x_sb")
            x_groups.append(x_sb)
        gain_row = const.tile([P, DIM], BF16)
        nc.gpsimd.memset(gain_row[:].bitcast(F32), 0.0)
        nc.sync.dma_start(out=gain_row[0:1, :], in_=attn_norm_w.rearrange("(o k) -> o k", o=1))
        nc.sync.dma_start(out=x_groups[0][:, 0, :], in_=x_view[:, 0, :])
        nc.sync.dma_start(out=x_groups[0][:, 1, :], in_=x_view[:, 1, :])
        early = {}
        for t in SCALAR_TILES:
            x_early = xearly.tile([P, DIM], BF16, name="x_early")
            early[t] = x_early

        def load_early(i):
            t = SCALAR_TILES[i]
            nc.sync.dma_start(out=early[t][:], in_=x_view[:, t, :])

        load_early(0)
        w_raw = const.tile([P, 4, DIM], BF16)
        nc.sync.dma_start(out=w_raw[:, 0, :], in_=wq_view[:, 1, :])
        nc.sync.dma_start(out=w_raw[:, 1, :], in_=wq_view[:, 0, :])
        nc.sync.dma_start(out=x_groups[0][:, PAIR:GROUP, :], in_=x_view[:, PAIR:GROUP, :])
        nc.sync.dma_start(out=w_raw[0:64, 2, :], in_=wk_view[:, 1, :])
        nc.sync.dma_start(out=w_raw[64:128, 2, :], in_=wk_view[:, 0, :])
        nc.sync.dma_start(out=w_raw[:, 3, :], in_=wv)
        load_early(1)
        nc.sync.dma_start(out=x_groups[1][:, 0:PAIR, :], in_=x_view[:, GROUP : GROUP + PAIR, :])
        cos_sb = const.tile([P, TILES, ANGLES], BF16)
        sin_sb = const.tile([P, TILES, ANGLES], BF16)
        nc.sync.dma_start(out=cos_sb[:], in_=cos_view)
        nc.sync.dma_start(out=sin_sb[:], in_=sin_view)
        nc.sync.dma_start(out=x_groups[1][:, PAIR:GROUP, :], in_=x_view[:, GROUP + PAIR : 2 * GROUP, :])
        load_early(2)
        load_early(3)
        for g in range(2, N_GROUPS):
            nc.sync.dma_start(out=x_groups[g][:], in_=x_view[:, g * GROUP : (g + 1) * GROUP, :])

        ident = const.tile([P, P], F32)
        make_identity(nc, ident[:])
        eps = const.tile([P, 1], F32)
        nc.vector.memset(eps[:], EPS)
        ones = const.tile([P, P], BF16)
        nc.vector.memset(ones[:], 1.0)
        plus = const.tile([P, P], BF16)
        nc.vector.tensor_copy(out=plus[:], in_=ident[:])
        minus = const.tile([P, P], BF16)
        nc.vector.tensor_scalar(minus[:], ident[:], -1.0, None, op0=ALU.mult)
        warm = const.tile([P, 1], F32)
        nc.scalar.activation(out=warm[:], in_=eps[:], func=ACT.Abs_reciprocal_sqrt)
        gain = ps_gain.tile([P, DIM], F32)
        nc.tensor.matmul(gain[:], lhsT=ones[:], rhs=gain_row[:], start=True, stop=True)
        gain_sb = const.tile([P, DIM], BF16)
        nc.vector.tensor_copy(out=gain_sb[:], in_=gain[:])
        scaled = {}
        for t in SCALAR_TILES:
            x_gain = xearly.tile([P, DIM], F32, name="x_gain")
            nc.gpsimd.tensor_tensor(out=x_gain[:], in0=early[t][:], in1=gain_sb[:], op=ALU.mult)
            scaled[t] = x_gain

        mix = const.tile([P, TILES, ANGLES, 2], F32)
        bank_of_part = {}

        def add_factors(part):
            lo, hi = part * MIX_TILES, (part + 1) * MIX_TILES
            cos_part = cos_sb[:, lo:hi, :].rearrange("p t j -> p (t j)")
            sin_part = sin_sb[:, lo:hi, :].rearrange("p t j -> p (t j)")
            bank = ps_eo.tile([P, 512], F32, name="bank")
            half = MIX_TILES * ANGLES
            nc.tensor.matmul(bank[:, 0:half], lhsT=minus[:], rhs=cos_part, start=True, stop=False)
            nc.tensor.matmul(bank[:, 0:half], lhsT=minus[:], rhs=sin_part, start=False, stop=True)
            nc.tensor.matmul(bank[:, half:], lhsT=minus[:], rhs=cos_part, start=True, stop=False)
            nc.tensor.matmul(bank[:, half:], lhsT=plus[:], rhs=sin_part, start=False, stop=True)
            bank_of_part[part] = bank

        def copy_factors(part):
            lo, hi = part * MIX_TILES, (part + 1) * MIX_TILES
            bank = bank_of_part.pop(part)
            nc.scalar.copy(
                out=mix[:, lo:hi, :, :].rearrange("p t j e -> p (t j) e"),
                in_=bank[:].rearrange("p (e n) -> p n e", e=2),
            )

        w_grouped = const.tile([P, W_COLS * 4], BF16, align_bytes=64)
        w_words = w_grouped[:].bitcast(F32).rearrange("p (n u) -> p n u", u=2)
        w_codes = const.tile([P, W_COLS], U32, align_bytes=64)
        w_scales = const.tile([P, W_COLS], U8, align_bytes=64)
        w_turned = []

        def turn_weights():
            for half in range(2):
                bank = ps_eo.tile([P, 512], F32, name="bank")
                w_t = bank[:].rearrange("p (a u n) -> p a u n", a=2, u=2)
                w_turned.append(w_t)
                for a in range(2):
                    for u in range(2):
                        nc.tensor.transpose(
                            w_t[:, a, u, :], w_raw[:, 2 * half + a, :].bitcast(F32)[:, u : 2 * P : 2], ident[:]
                        )

        def quantise_weights():
            rope = w_words[:, 0:V_AT, :].rearrange("p (a n) u -> p a n u", a=2)
            nc.vector.tensor_copy(out=rope[:, :, 0:P, :], in_=w_turned[0].rearrange("p a u n -> p a n u"))
            nc.vector.tensor_copy(
                out=rope[:, :, P:HALF, :], in_=w_turned[1][:, 0, :, :].rearrange("p u (a n) -> p a n u", a=2)
            )
            nc.vector.tensor_copy(
                out=w_words[:, V_AT:, :], in_=w_turned[1][:, 1, :, :].rearrange("p u n -> p n u")
            )
            nc.vector.quantize_mx(out=w_codes[:].bitcast(FP8X4), scales=w_scales[:], in_=w_grouped[:])

        sums_of_batch = {}
        rstd_of_tile = {}
        normed_of_pair = {}
        turned_of_pair = {}
        codes_of_pair = {}
        h_of_pair = {}
        banks_of_pair = {}
        outs_of_group = {}
        products_of_group = {}

        def batch_of(t):
            count = 1 if t < GROUP else PAIR if t < 2 * GROUP else GROUP
            return t - t % count, count

        def squares(pair, members=range(PAIR)):
            for a in members:
                t = pair * PAIR + a
                g, at = divmod(t, GROUP)
                first, count = batch_of(t)
                if t == first:
                    sumsq = stats.tile([P, GROUP], F32, name="sumsq")
                    sums_of_batch[first] = sumsq
                junk = stats.tile([P, DIM], BF16, name="junk")
                nc.scalar.activation(
                    out=junk[:], in_=x_groups[g][:, at, :], func=ACT.Square,
                    accum_out=sums_of_batch[first][:, t - first : t - first + 1],
                )
                if t + 1 == first + count:
                    rstd = stats.tile([P, GROUP], F32, name="rstd")
                    nc.scalar.activation(
                        out=rstd[:, 0:count], in_=sums_of_batch.pop(first)[:, 0:count],
                        func=ACT.Abs_reciprocal_sqrt, bias=eps[:], scale=1.0 / DIM,
                    )
                    for i in range(count):
                        rstd_of_tile[first + i] = rstd[:, i : i + 1]

        def normalise_on_scalar(pair):
            h = work.tile([P, PAIR, DIM], BF16, name="h")
            for a in range(PAIR):
                t = pair * PAIR + a
                if t in scaled:
                    nc.scalar.activation(
                        out=h[:, a, :], in_=scaled[t][:], func=ACT.Copy, scale=rstd_of_tile.pop(t)
                    )
            normed_of_pair[pair] = h

        def normalise(pair):
            if pair not in normed_of_pair:
                normalise_on_scalar(pair)
            h = normed_of_pair.pop(pair)
            turned = ps_t.tile([P, PAIR, 2, P], F32, tag="turned")
            for a in range(PAIR):
                t = pair * PAIR + a
                g, at = divmod(t, GROUP)
                if t not in scaled:
                    nc.vector.scalar_tensor_tensor(
                        out=h[:, a, :], in0=x_groups[g][:, at, :], scalar=rstd_of_tile.pop(t), in1=gain[:],
                        op0=ALU.mult, op1=ALU.mult,
                    )
                for u in range(2):
                    nc.tensor.transpose(
                        turned[:, a, u, :], h[:, a, :].bitcast(F32)[:, u : 2 * P : 2], ident[:]
                    )
            turned_of_pair[pair] = turned

        def words(pair):
            h_grouped = work.tile([P, PAIR * P * 4], BF16, name="h_grouped", align_bytes=64)
            nc.scalar.copy(
                out=h_grouped[:].bitcast(F32).rearrange("p (a r u) -> p a r u", a=PAIR, u=2),
                in_=turned_of_pair.pop(pair)[:].rearrange("p a u r -> p a r u"),
            )
            h_of_pair[pair] = h_grouped

        def quantise(pair):
            codes = work.tile([P, PAIR * P], U32, name="codes", align_bytes=64)
            scales = work.tile([P, PAIR * P], U8, name="scales", align_bytes=64)
            nc.vector.quantize_mx(out=codes[:].bitcast(FP8X4), scales=scales[:], in_=h_of_pair.pop(pair)[:])
            codes_of_pair[pair] = (codes, scales)

        def project(pair):
            codes, scales = codes_of_pair.pop(pair)

            def one_pass(dest, a, lo, hi, start, stop):
                tokens = slice(a * P, (a + 1) * P)
                nc.tensor.matmul_mx(
                    out=dest,
                    lhsT=codes[:, tokens].bitcast(FP8X4),
                    lhsT_scale=scales[:, tokens],
                    rhs=w_codes[:, lo:hi].bitcast(FP8X4),
                    rhs_scale=w_scales[:, lo:hi],
                    start=start,
                    stop=stop,
                )

            sums = ps_sum.tile([P, PAIR, 256], F32, name="sums")
            v_bank = ps_v.tile([P, PAIR, 2 * KV_COLS], F32, name="v_bank")
            members = []
            for a in range(PAIR):
                one_pass(sums[:, a, :], a, 0, 256, True, False)
                one_pass(sums[:, a, :], a, HALF, HALF + 256, False, True)
            for a in range(PAIR):
                bank = ps_eo.tile([P, 512], F32, name="bank")
                members.append(bank)
                one_pass(bank[:, 0:256], a, 0, 256, True, True)
                one_pass(bank[:, 256 : 2 * HALF], a, 256, 2 * HALF, True, True)
                one_pass(v_bank[:, a, :], a, V_AT - KV_COLS, V_AT + KV_COLS, True, True)
            banks_of_pair[pair] = (sums, v_bank, members)

        def copy_v(pair):
            g, first = divmod(pair * PAIR, GROUP)
            if first == 0:
                turned_out = outs.tile([P, GROUP, 2 * HALF], F32, name="turned_out")
                v_out = outs.tile([P, GROUP, KV_COLS], F32, name="v_out")
                outs_of_group[g] = (turned_out, v_out)
            nc.scalar.copy(out=outs_of_group[g][1][:, first : first + PAIR, :], in_=banks_of_pair[pair][1][:, :, KV_COLS:])

        def common_products(pair):
            t0 = pair * PAIR
            first = t0 % GROUP
            if first == 0:
                common = work.tile([P, GROUP, HALF], F32, name="common")
                own = work.tile([P, GROUP, 2 * HALF], F32, name="own")
                products_of_group[t0 // GROUP] = (common, own)
            common = products_of_group[t0 // GROUP][0]
            nc.vector.tensor_tensor(
                out=common[:, first : first + PAIR, :].rearrange("p a (h j) -> p a h j", j=ANGLES),
                in0=banks_of_pair[pair][0][:, :, 0:HALF].rearrange("p a (h j) -> p a h j", j=ANGLES),
                in1=cos_sb[:, t0 : t0 + PAIR, :].unsqueeze(2).to_broadcast([P, PAIR, HEADS, ANGLES]),
                op=ALU.mult,
            )

        def own_products(tile):
            g, at = divmod(tile, GROUP)
            bank = banks_of_pair[tile // PAIR][2][tile % PAIR]
            nc.vector.tensor_tensor(
                out=products_of_group[g][1][:, at, :].rearrange("p (h j e) -> p h j e", h=HEADS, e=2),
                in0=bank[:, 0 : 2 * HALF].rearrange("p (e h j) -> p h j e", e=2, h=HEADS),
                in1=mix[:, tile, :, :].unsqueeze(1).to_broadcast([P, HEADS, ANGLES, 2]),
                op=ALU.mult,
            )

        def is_late(pair):
            return pair + 3 >= N_PAIRS

        def add_products(tile):
            g, at = divmod(tile, GROUP)
            common, own = products_of_group[g]
            engine = nc.vector if is_late(tile // PAIR) and tile % PAIR == 1 else nc.gpsimd
            engine.tensor_tensor(
                out=outs_of_group[g][0][:, at, :].rearrange("p (n e) -> p n e", e=2),
                in0=own[:, at, :].rearrange("p (n e) -> p n e", e=2),
                in1=common[:, at, :].unsqueeze(2).to_broadcast([P, HALF, 2]),
                op=ALU.add,
            )

        def store_v(first_tile, count):
            g, at = divmod(first_tile, GROUP)
            tiles = slice(first_tile, first_tile + count)
            nc.sync.dma_start(out=v_view[:, tiles, :], in_=outs_of_group[g][1][:, at : at + count, :])

        def store_q_and_k(first_tile, count):
            g, at = divmod(first_tile, GROUP)
            tiles, here = slice(first_tile, first_tile + count), slice(at, at + count)
            turned_out = outs_of_group[g][0]
            nc.sync.dma_start(out=q_view[:, tiles, :], in_=turned_out[:, here, 0:Q_COLS])
            nc.sync.dma_start(out=k_view[:, tiles, :], in_=turned_out[:, here, Q_COLS:])

        def add_and_store(pair, members=range(PAIR)):
            t0 = pair * PAIR
            for a in members:
                add_products(t0 + a)
            done = t0 + members[-1] + 1
            if pair == N_PAIRS - 1:
                if done < TILES:
                    store_v(t0, PAIR)
                store_q_and_k(done - 1, 1)
            elif pair == N_PAIRS - 2:
                if done % PAIR == 0:
                    store_v(t0, PAIR)
                    store_q_and_k(t0, PAIR)
            elif done % GROUP == 0:
                store_v(done - GROUP, GROUP)
                store_q_and_k(done - GROUP, GROUP)

        def on(stage, pair, *more):
            if 0 <= pair < N_PAIRS:
                stage(pair, *more)

        squares(0)
        squares(1)
        turn_weights()
        normalise(0)
        words(0)
        squares(2)
        add_factors(0)
        copy_factors(0)
        quantise_weights()
        quantise(0)
        project(0)
        normalise(1)
        squares(3)
        words(1)
        normalise(2)
        squares(4)
        for s in range(N_PAIRS):
            copy_v(s)
            if s + 3 >= N_PAIRS:
                on(quantise, s + 1)
            common_products(s)
            own_products(s * PAIR)
            if s + 3 < N_PAIRS:
                on(quantise, s + 1)
            if is_late(s - 1):
                add_and_store(s - 1, [1])
            own_products(s * PAIR + 1)
            on(project, s + 1)
            on(squares, s + 5, [0])
            on(words, s + 2)
            if s - 1 in FACTOR_STEPS:
                copy_factors(1 + FACTOR_STEPS.index(s - 1))
            on(squares, s + 5, [1])
            on(normalise, s + 3)
            if s + 4 in SCALAR_PAIRS:
                normalise_on_scalar(s + 4)
            if s in FACTOR_STEPS:
                add_factors(1 + FACTOR_STEPS.index(s))
            add_and_store(s, [0] if is_late(s) else range(PAIR))
        add_and_store(N_PAIRS - 1, [1])
